import numpy as np
import ml_dtypes


def mxq(x, axis, fmt="e4m3"):
    dtype, down = {"e4m3": (ml_dtypes.float8_e4m3fn, 7), "e5m2": (ml_dtypes.float8_e5m2, 14)}[fmt]
    v = np.moveaxis(np.asarray(x, np.float32).astype(ml_dtypes.bfloat16).astype(np.float64), axis, -1)
    blocks = v.reshape(v.shape[:-1] + (-1, 32))
    amax = np.abs(blocks).max(-1, keepdims=True)
    byte = np.maximum(np.where(amax > 0, np.frexp(amax)[1] - 1 + 127, 0) - down, 1)
    scale = np.exp2(byte - 127.0)
    codes = (blocks / scale).astype(np.float32).astype(dtype).astype(np.float64)
    return np.moveaxis((codes * scale).reshape(v.shape), -1, axis)


WIDE = False


def mx_kscale(k):
    if not WIDE:
        return np.ones(k)
    levels = np.array([10, -10, 5, -5, 0])
    if k % 512:
        return np.exp2(np.random.permutation(np.resize(levels, k // 32))).repeat(32)
    a = np.empty((k // 512, 16))
    for p in range(k // 512):
        a[p, :8] = np.random.permutation(np.resize(levels, 8))
        for g in range(8):
            far = levels[np.abs(levels - a[p, g]) >= 10]
            a[p, g + 8] = far[np.random.randint(len(far))]
    return np.exp2(a.ravel()).repeat(32)


BF16 = ml_dtypes.bfloat16


def bf(x):
    return np.asarray(x, np.float32).astype(BF16)


def f64(x):
    return np.asarray(x).astype(np.float64)


B, IN, L = 256, 2048, 1536


def sigmoid(v):
    return 1.0 / (1.0 + np.exp(-v))


def setup_inputs():
    s = mx_kscale(IN)
    return {"input": bf(np.random.standard_normal((B, IN)) * s),
            "h0": bf(np.random.standard_normal((B, L))),
            "gh0": bf(np.random.standard_normal((B, 3 * L)) * 0.75),
            "W_ih0": bf(np.random.standard_normal((3 * L, IN)) * 0.7 / np.sqrt(IN) / s),
            "b_ih0": bf(np.random.standard_normal(3 * L) * 0.3)}


def core(input, h0, gh0, W_ih0, b_ih0):
    h, gh = f64(h0), f64(gh0)
    gi = (mxq(f64(input), 1, "e4m3") @ mxq(f64(W_ih0), 1, "e4m3").T) + f64(b_ih0)
    i_r, i_z, i_n = gi[:, :L], gi[:, L:2 * L], gi[:, 2 * L:]
    h_r, h_z, h_n = gh[:, :L], gh[:, L:2 * L], gh[:, 2 * L:]
    r = sigmoid(i_r + h_r)
    z = sigmoid(i_z + h_z)
    n = np.tanh(i_n + r * h_n)
    return (1.0 - z) * n + z * h


def e4m3fn_bytes(y):
    return np.clip(np.asarray(y, np.float64), -448.0, 448.0).astype(np.float32).astype(ml_dtypes.float8_e4m3fn).view(np.uint8)


def reference(input, h0, gh0, W_ih0, b_ih0):
    out = core(input, h0, gh0, W_ih0, b_ih0)
    s = np.max(np.abs(out)) / 448.0
    return out, e4m3fn_bytes(out / s)

@@ -1,0 +1,336 @@
+from contextlib import ExitStack
+
+import concourse.mybir as mybir
+from concourse.masks import make_identity
+
+B, IN, L = 256, 2048, 1536
+FLOPS = 2 * B * IN * 3 * L
+
+F32 = mybir.dt.float32
+BF16 = mybir.dt.bfloat16
+U32 = mybir.dt.uint32
+U8 = mybir.dt.uint8
+FP8X4 = mybir.dt.float8_e4m3fn_x4
+FP8 = mybir.dt.float8_e4m3fn
+ALU = mybir.AluOpType
+ACT = mybir.ActivationFunctionType
+AX = mybir.AxisListType
+
+P = 128
+NB = 2
+NG = 4
+CB = 256
+NCB = L // CB
+NPAIR = 3 * NCB
+AHEAD = 7
+
+
+def tile_grucellstack_pa_kernel(tc, x, h0, gh0, w_ih, b_ih, out_0, out_1):
+    nc = tc.nc
+    with ExitStack() as ctx:
+        const = ctx.enter_context(tc.tile_pool(name="const", bufs=1))
+        raw = ctx.enter_context(tc.tile_pool(name="raw", bufs=16))
+        grp_pool = ctx.enter_context(tc.tile_pool(name="grp", bufs=4))
+        code_pool = ctx.enter_context(tc.tile_pool(name="code", bufs=3))
+        tmp = ctx.enter_context(tc.tile_pool(name="tmp", bufs=2))
+        tp_pool = ctx.enter_context(tc.psum_pool(name="tp", bufs=4))
+        acc_pool = ctx.enter_context(tc.psum_pool(name="acc", bufs=4))
+        ctx.enter_context(tc.manual_schedule())
+
+        zeros = const.tile([P, 1], F32, name="zeros")
+        nc.vector.memset(zeros[:], 0.0)
+        junk = const.tile([P, 1], F32, name="junk")
+        nc.scalar.activation(out=junk[:], in_=zeros[:], func=ACT.Tanh)
+        ident = const.tile([P, P], F32, name="ident")
+        make_identity(nc, ident[:])
+
+        xc = const.tile([P, NG, 2 * P], U32, name="xc", align_bytes=64)
+        xs = const.tile([P, NG, 2 * P], U8, name="xs", align_bytes=64)
+        o_all = const.tile([P, NB, L], F32, name="o_all")
+        pm = const.tile([P, 8], F32, name="pm")
+
+        gh_v = gh0.rearrange("(b p) (g l) -> b p g l", p=P, g=3)
+        h_v = h0.rearrange("(b p) l -> p b l", p=P)
+        b_v = b_ih.rearrange("(g l) -> g l", g=3)
+        o0_v = out_0.rearrange("(b p) l -> p b l", p=P)
+
+        raw_tiles = {}
+        gh_t = {}
+        h_t = {}
+        b_t = {}
+
+        def load_pair(q):
+            tiles = []
+            for j in range(2):
+                t = raw.tile([P, IN], BF16, name="rawt", tag="raw")
+                if q < 0:
+                    src = x[P * j:P * (j + 1), :]
+                else:
+                    n0 = (q % 3) * L + (q // 3) * CB + P * j
+                    src = w_ih[n0:n0 + P, :]
+                nc.sync.dma_start(out=t[:], in_=src)
+                tiles.append(t)
+            raw_tiles[q] = tiles
+
+        def load_bias(k):
+            t = const.tile([P, 3, 512], BF16, name="bias%d" % k)
+            nc.sync.dma_start(out=t[:], in_=b_v[:, 512 * k:512 * (k + 1)].partition_broadcast(P))
+            b_t[k] = t
+
+        def load_gh(k):
+            t = const.tile([P, NB, 3, 512], BF16, name="gh%d" % k)
+            for b in range(NB):
+                nc.sync.dma_start(out=t[:, b, :, :], in_=gh_v[b, :, :, 512 * k:512 * (k + 1)])
+            gh_t[k] = t
+
+        def load_h(k):
+            t = const.tile([P, NB, 512], BF16, name="h%d" % k)
+            nc.sync.dma_start(out=t[:], in_=h_v[:, :, 512 * k:512 * (k + 1)])
+            h_t[k] = t
+
+        def run(fns):
+            for fn in fns:
+                fn()
+
+        def stage(q, codes, scales, by_tile, slots):
+            words = [t[:].bitcast(F32) for t in raw_tiles[q]]
+            banks = []
+
+            def new_bank():
+                bk = tp_pool.tile([P, 2, 2 * P], F32, name="bank", tag="tp")
+                banks.append(bk)
+
+            def tr(g, j):
+                for u in range(2):
+                    nc.tensor.transpose(
+                        banks[g][:, u, P * j:P * (j + 1)],
+                        words[j][:, 256 * g + u:256 * (g + 1):2],
+                        ident[:],
+                    )
+
+            if by_tile:
+                for g in range(NG):
+                    new_bank()
+                for j in range(2):
+                    for g in range(NG):
+                        tr(g, j)
+            gts = []
+            for g in range(NG):
+                if not by_tile:
+                    new_bank()
+                    tr(g, 0)
+                    tr(g, 1)
+                if g % 2 == 0:
+                    gt = grp_pool.tile([P, 2, 1024], BF16, name="gt", tag="grp", align_bytes=64)
+                    gts.append(gt)
+                nc.scalar.copy(
+                    out=gts[-1][:, g % 2, :].bitcast(F32).rearrange("p (r u) -> p r u", u=2),
+                    in_=banks[g][:].rearrange("p u r -> p r u"),
+                )
+                if g % 2 == 1:
+                    if g == 1:
+                        run(slots.get("a", []))
+                        run(slots.get("b", []))
+                        run(slots.get("c", []))
+                    else:
+                        run(slots.get("d", []))
+                    nc.vector.quantize_mx(
+                        out=codes[:, g - 1:g + 1, :].rearrange("p g r -> p (g r)").bitcast(FP8X4),
+                        scales=scales[:, g - 1:g + 1, :].rearrange("p g r -> p (g r)"),
+                        in_=gts[-1][:].rearrange("p g c -> p (g c)"),
+                    )
+            run(slots.get("e", []))
+
+        wcodes = {}
+        acc = {}
+
+        def new_codes(q):
+            c_t = code_pool.tile([P, NG, 2 * P], U32, name="wc", tag="wc", align_bytes=64)
+            s_t = code_pool.tile([P, NG, 2 * P], U8, name="ws", tag="ws", align_bytes=64)
+            wcodes[q] = (c_t, s_t)
+            return c_t, s_t
+
+        def mx(q):
+            c_t, s_t = wcodes[q]
+            a_t = acc_pool.tile([P, NB, CB], F32, name="acc", tag="acc")
+            acc[q] = a_t
+            for b in range(NB):
+                for g in range(NG):
+                    nc.tensor.matmul_mx(
+                        out=a_t[:, b, :],
+                        lhsT=xc[:, g, P * b:P * (b + 1)].bitcast(FP8X4),
+                        lhsT_scale=xs[:, g, P * b:P * (b + 1)],
+                        rhs=c_t[:, g, :].bitcast(FP8X4),
+                        rhs_scale=s_t[:, g, :],
+                        start=(g == 0),
+                        stop=(g == NG - 1),
+                    )
+
+        st = {}
+        ALLB = slice(0, NB)
+
+        def cols(c):
+            return slice(CB * (c % 2), CB * (c % 2) + CB)
+
+        def ghv(c, gate, bs):
+            return gh_t[c // 2][:, bs, gate, cols(c)]
+
+        def bv(c, gate, bs):
+            return b_t[c // 2][:, gate, cols(c)].unsqueeze(1).to_broadcast([P, bs.stop - bs.start, CB])
+
+        def tl(nm, c):
+            if (nm, c) not in st:
+                t = tmp.tile([P, NB, CB], F32, name=nm, tag=nm)
+                st[(nm, c)] = t
+            return st[(nm, c)]
+
+        def pre(c, gate):
+            nc.vector.tensor_tensor(out=tl("G%d" % gate, c)[:], in0=ghv(c, gate, ALLB), in1=bv(c, gate, ALLB), op=ALU.add)
+
+        def e12(c, gate):
+            nc.vector.tensor_tensor(out=tl("a%d" % gate, c)[:], in0=acc[3 * c + gate][:], in1=tl("G%d" % gate, c)[:], op=ALU.add)
+
+        def s12(c, gate):
+            nc.scalar.activation(out=tl("th%d" % gate, c)[:], in_=tl("a%d" % gate, c)[:], func=ACT.Tanh, scale=0.5)
+
+        def e3(c):
+            nc.vector.scalar_tensor_tensor(out=tl("w", c)[:], in0=tl("th0", c)[:], scalar=1.0, in1=ghv(c, 2, ALLB), op0=ALU.add, op1=ALU.mult)
+
+        def e4(c, bs=ALLB):
+            nc.vector.tensor_tensor(out=tl("v", c)[:, bs, :], in0=acc[3 * c + 2][:, bs, :], in1=bv(c, 2, bs), op=ALU.add)
+
+        def e5(c, bs=ALLB):
+            nc.vector.scalar_tensor_tensor(out=tl("u", c)[:, bs, :], in0=tl("w", c)[:, bs, :], scalar=0.5, in1=tl("v", c)[:, bs, :], op0=ALU.mult, op1=ALU.add)
+
+        def s3(c, bs=ALLB):
+            nc.scalar.activation(out=tl("n", c)[:, bs, :], in_=tl("u", c)[:, bs, :], func=ACT.Tanh)
+
+        def e6(c, bs=ALLB):
+            nc.vector.tensor_tensor(out=tl("d", c)[:, bs, :], in0=h_t[c // 2][:, bs, cols(c)], in1=tl("n", c)[:, bs, :], op=ALU.subtract)
+
+        def e7(c, bs=ALLB):
+            nc.vector.scalar_tensor_tensor(out=tl("e", c)[:, bs, :], in0=tl("th1", c)[:, bs, :], scalar=1.0, in1=tl("d", c)[:, bs, :], op0=ALU.add, op1=ALU.mult)
+
+        def e8(c, bs=ALLB):
+            nc.vector.scalar_tensor_tensor(out=o_all[:, bs, CB * c:CB * (c + 1)], in0=tl("e", c)[:, bs, :], scalar=0.5, in1=tl("n", c)[:, bs, :], op0=ALU.mult, op1=ALU.add)
+
+        def store0(c):
+            nc.sync.dma_start(out=o0_v[:, :, CB * c:CB * (c + 1)], in_=o_all[:, :, CB * c:CB * (c + 1)])
+
+        def e9(col, b, lo, hi):
+            nc.vector.tensor_reduce(out=pm[:, col:col + 1], in_=o_all[:, b, lo:hi], axis=AX.X, op=ALU.max, apply_absolute_value=True)
+
+        plan = {}
+
+        def at(it, slot, fn):
+            plan.setdefault(it, {}).setdefault(slot, []).append(fn)
+
+        for c in range(NCB):
+            if c == 0:
+                at(1, "e", lambda c=c: pre(c, 0))
+                at(1, "e", lambda c=c: pre(c, 1))
+                at(2, "a", lambda c=c: e12(c, 0))
+                at(2, "b", lambda c=c: e12(c, 1))
+                at(2, "s", lambda c=c: s12(c, 0))
+                at(2, "s", lambda c=c: s12(c, 1))
+                at(3, "a", lambda c=c: e4(c))
+                at(3, "b", lambda c=c: e3(c))
+                at(3, "d", lambda c=c: e5(c))
+            else:
+                if c == 1:
+                    at(3, "c", lambda c=c: pre(c, 0))
+                    at(4, "c", lambda c=c: pre(c, 1))
+                else:
+                    at(3 * c, "b", lambda c=c: pre(c, 0))
+                    at(3 * c, "d", lambda c=c: pre(c, 1))
+                at(3 * c + 1, "a", lambda c=c: e12(c, 0))
+                at(3 * c + 1, "s", lambda c=c: s12(c, 0))
+                if c < NCB - 1:
+                    at(3 * c + 2, "a", lambda c=c: e12(c, 1))
+                    at(3 * c + 2, "s", lambda c=c: s12(c, 1))
+                    at(3 * c + 2, "c", lambda c=c: e3(c))
+                    at(3 * c + 3, "a", lambda c=c: e4(c))
+                    at(3 * c + 3, "c", lambda c=c: e5(c))
+            if c < NCB - 1:
+                at(3 * c + 3, "s", lambda c=c: s3(c))
+                at(3 * c + 4, "b", lambda c=c: e6(c))
+                at(3 * c + 4, "d", lambda c=c: e7(c))
+            if c < NCB - 2:
+                at(3 * c + 5, "b", lambda c=c: e8(c))
+                at(3 * c + 5, "b", lambda c=c: store0(c))
+                if c % 2 == 1:
+                    at(3 * c + 5, "d", lambda c=c: e9(c - 1, 0, CB * (c - 1), CB * (c + 1)))
+                    at(3 * c + 7, "c", lambda c=c: e9(c, 1, CB * (c - 1), CB * (c + 1)))
+
+        load_pair(-1)
+        load_pair(0)
+        load_pair(1)
+        load_bias(0)
+        load_pair(2)
+        load_gh(0)
+        load_pair(3)
+        load_h(0)
+        load_pair(4)
+        load_pair(5)
+        load_pair(6)
+        load_bias(1)
+        load_gh(1)
+        load_h(1)
+
+        stage(-1, xc, xs, True, {})
+        c_t, s_t = new_codes(0)
+        stage(0, c_t, s_t, True, {})
+
+        for it in range(NPAIR - 1):
+            if it + AHEAD < NPAIR:
+                load_pair(it + AHEAD)
+            if it == 3:
+                load_bias(2)
+                load_gh(2)
+                load_h(2)
+            c_t, s_t = new_codes(it + 1)
+            stage(it + 1, c_t, s_t, it + 1 <= 2, plan.get(it, {}))
+            mx(it)
+            run(plan.get(it, {}).get("s", []))
+
+        c = NCB - 1
+        halves = [slice(0, 1), slice(1, 2)]
+        mx(NPAIR - 1)
+        e12(c, 1)
+        s12(c, 1)
+        e3(c)
+        e8(c - 1)
+        store0(c - 1)
+        for bs in halves:
+            e4(c, bs)
+        for bs in halves:
+            e5(c, bs)
+        for bs in halves:
+            s3(c, bs)
+        for b in range(NB):
+            e9(4 + b, b, CB * (c - 1), CB * c)
+        for fn in (e6, e7, e8):
+            for bs in halves:
+                fn(c, bs)
+        for b in range(NB):
+            e9(6 + b, b, CB * c, CB * (c + 1))
+        store0(c)
+
+        pmx = const.tile([P, 1], F32, name="pmx")
+        nc.vector.tensor_reduce(out=pmx[:], in_=pm[:], axis=AX.X, op=ALU.max)
+        spread = tp_pool.tile([P, 2, 2 * P], F32, name="bank", tag="tp")
+        nc.tensor.transpose(spread[:, 0, 0:P], pmx[:, 0:1].to_broadcast([P, P]), ident[:])
+        amax = const.tile([P, 1], F32, name="amax")
+        nc.vector.tensor_reduce(out=amax[:], in_=spread[:, 0, 0:P], axis=AX.X, op=ALU.max)
+        rec = const.tile([P, 1], F32, name="rec")
+        nc.vector.reciprocal(out=rec[:], in_=amax[:])
+        rs = const.tile([P, 1], F32, name="rs")
+        nc.vector.tensor_scalar(out=rs[:], in0=rec[:], scalar1=448.0, scalar2=None, op0=ALU.mult)
+
+        f8a = const.tile([P, L], FP8, name="f8a")
+        f8b = const.tile([P, L], FP8, name="f8b")
+        nc.scalar.activation(out=f8b[:, 512:L], in_=o_all[:, 1, 512:L], func=ACT.Identity, scale=rs[:, 0:1], bias=zeros[:, 0:1], saturate=False)
+        nc.vector.tensor_scalar(out=f8a[:], in0=o_all[:, 0, :], scalar1=rs[:, 0:1], scalar2=None, op0=ALU.mult, saturate=False)
+        nc.sync.dma_start(out=out_1[0:P, :], in_=f8a[:].bitcast(U8))
+        nc.vector.tensor_scalar(out=f8b[:, 0:512], in0=o_all[:, 1, 0:512], scalar1=rs[:, 0:1], scalar2=None, op0=ALU.mult, saturate=False)
+        nc.sync.dma_start(out=out_1[P:2 * P, :], in_=f8b[:].bitcast(U8))

@@ -8,6 +8,7 @@ FLOPS = 2 * B * IN * 3 * L
 
 F32 = mybir.dt.float32
 BF16 = mybir.dt.bfloat16
+I32 = mybir.dt.int32
 U32 = mybir.dt.uint32
 U8 = mybir.dt.uint8
 FP8X4 = mybir.dt.float8_e4m3fn_x4
@@ -23,26 +24,36 @@ CB = 256
 NCB = L // CB
 NPAIR = 3 * NCB
 AHEAD = 7
+PAIRS = [(g, c) for c in range(NCB - 2) for g in range(3)] + [(0, 4), (0, 5), (1, 4), (2, 4), (1, 5), (2, 5)]
+SPLIT_MX = False
+NWARM = 6
 
 
 def tile_grucellstack_pa_kernel(tc, x, h0, gh0, w_ih, b_ih, out_0, out_1):
     nc = tc.nc
     with ExitStack() as ctx:
         const = ctx.enter_context(tc.tile_pool(name="const", bufs=1))
-        raw = ctx.enter_context(tc.tile_pool(name="raw", bufs=16))
+        raw = ctx.enter_context(tc.tile_pool(name="raw", bufs=8))
         grp_pool = ctx.enter_context(tc.tile_pool(name="grp", bufs=4))
         code_pool = ctx.enter_context(tc.tile_pool(name="code", bufs=3))
         tmp = ctx.enter_context(tc.tile_pool(name="tmp", bufs=2))
         tp_pool = ctx.enter_context(tc.psum_pool(name="tp", bufs=4))
-        acc_pool = ctx.enter_context(tc.psum_pool(name="acc", bufs=4))
+        acc_pool = ctx.enter_context(tc.psum_pool(name="acc", bufs=2))
+        bias_pool = ctx.enter_context(tc.psum_pool(name="biasp", bufs=2))
         ctx.enter_context(tc.manual_schedule())
 
         zeros = const.tile([P, 1], F32, name="zeros")
         nc.vector.memset(zeros[:], 0.0)
         junk = const.tile([P, 1], F32, name="junk")
         nc.scalar.activation(out=junk[:], in_=zeros[:], func=ACT.Tanh)
+        onesw = const.tile([P, 512], BF16, name="onesw")
+        nc.gpsimd.memset(onesw[:], 1.0)
+        bias_rows = const.tile([P, 3 * CB], BF16, name="bias_rows")
+        nc.vector.memset(bias_rows[:].bitcast(I32), 0)
         ident = const.tile([P, P], F32, name="ident")
         make_identity(nc, ident[:])
+        identb = const.tile([P, P], BF16, name="identb")
+        make_identity(nc, identb[:])
 
         xc = const.tile([P, NG, 2 * P], U32, name="xc", align_bytes=64)
         xs = const.tile([P, NG, 2 * P], U8, name="xs", align_bytes=64)
@@ -51,31 +62,26 @@ def tile_grucellstack_pa_kernel(tc, x, h0, gh0, w_ih, b_ih, out_0, out_1):
 
         gh_v = gh0.rearrange("(b p) (g l) -> b p g l", p=P, g=3)
         h_v = h0.rearrange("(b p) l -> p b l", p=P)
-        b_v = b_ih.rearrange("(g l) -> g l", g=3)
         o0_v = out_0.rearrange("(b p) l -> p b l", p=P)
 
         raw_tiles = {}
         gh_t = {}
         h_t = {}
-        b_t = {}
 
-        def load_pair(q):
-            tiles = []
-            for j in range(2):
-                t = raw.tile([P, IN], BF16, name="rawt", tag="raw")
-                if q < 0:
-                    src = x[P * j:P * (j + 1), :]
-                else:
-                    n0 = (q % 3) * L + (q // 3) * CB + P * j
-                    src = w_ih[n0:n0 + P, :]
+        def load_pair(q, split):
+            t = raw.tile([P, 2, IN], BF16, name="rawt", tag="raw")
+            if q < 0:
+                src = x
+            else:
+                n0 = PAIRS[q][0] * L + PAIRS[q][1] * CB
+                src = w_ih[n0:n0 + 2 * P, :]
+            src = src.rearrange("(j p) k -> p j k", p=P)
+            if split:
+                for s in range(2):
+                    nc.sync.dma_start(out=t[:, :, 1024 * s:1024 * (s + 1)], in_=src[:, :, 1024 * s:1024 * (s + 1)])
+            else:
                 nc.sync.dma_start(out=t[:], in_=src)
-                tiles.append(t)
-            raw_tiles[q] = tiles
-
-        def load_bias(k):
-            t = const.tile([P, 3, 512], BF16, name="bias%d" % k)
-            nc.sync.dma_start(out=t[:], in_=b_v[:, 512 * k:512 * (k + 1)].partition_broadcast(P))
-            b_t[k] = t
+            raw_tiles[q] = t
 
         def load_gh(k):
             t = const.tile([P, NB, 3, 512], BF16, name="gh%d" % k)
@@ -88,45 +94,55 @@ def tile_grucellstack_pa_kernel(tc, x, h0, gh0, w_ih, b_ih, out_0, out_1):
             nc.sync.dma_start(out=t[:], in_=h_v[:, :, 512 * k:512 * (k + 1)])
             h_t[k] = t
 
+        bias_ps = {}
+
+        def bias_mm(c, gate):
+            ps = bias_pool.tile([P, NB, CB], F32, name="bps", tag="bps")
+            nc.tensor.matmul(out=ps[:, 0, :], lhsT=identb[:, c:c + 1].to_broadcast([P, P]), rhs=bias_rows[:, CB * gate:CB * (gate + 1)], start=True, stop=True)
+            bias_ps[(c, gate)] = ps
+
+        def bv(c, gate):
+            return bias_ps[(c, gate)][:, 0:1, :].to_broadcast([P, NB, CB])
+
+        idle = acc_pool.tile([P, NB, CB], F32, name="acc", tag="acc")
+
+        def idle_mm(n):
+            nc.tensor.matmul(out=idle[:].rearrange("p b c -> p (b c)")[:, 0:n], lhsT=onesw[:, 0:P], rhs=onesw[:, 0:n], start=True, stop=True)
+
         def run(fns):
             for fn in fns:
                 fn()
 
-        def stage(q, codes, scales, by_tile, slots):
-            words = [t[:].bitcast(F32) for t in raw_tiles[q]]
-            banks = []
+        def nothing(i):
+            return None
 
-            def new_bank():
-                bk = tp_pool.tile([P, 2, 2 * P], F32, name="bank", tag="tp")
-                banks.append(bk)
-
-            def tr(g, j):
-                for u in range(2):
-                    nc.tensor.transpose(
-                        banks[g][:, u, P * j:P * (j + 1)],
-                        words[j][:, 256 * g + u:256 * (g + 1):2],
-                        ident[:],
-                    )
-
-            if by_tile:
-                for g in range(NG):
-                    new_bank()
-                for j in range(2):
-                    for g in range(NG):
-                        tr(g, j)
+        def stage(q, codes, scales, slots, v_helps, mx_half):
+            words = [raw_tiles[q][:, j, :].bitcast(F32) for j in range(2)]
             gts = []
             for g in range(NG):
-                if not by_tile:
-                    new_bank()
-                    tr(g, 0)
-                    tr(g, 1)
+                bank = tp_pool.tile([P, 2, 2 * P], F32, name="bank", tag="tp")
+                for j in range(2):
+                    for u in range(2):
+                        nc.tensor.transpose(
+                            bank[:, u, P * j:P * (j + 1)],
+                            words[j][:, 256 * g + u:256 * (g + 1):2],
+                            ident[:],
+                        )
+                if g == 1:
+                    run(slots.get("pe", []))
+                    mx_half(0)
+                if g == 3:
+                    run(slots.get("pe2", []))
+                    mx_half(1)
                 if g % 2 == 0:
                     gt = grp_pool.tile([P, 2, 1024], BF16, name="gt", tag="grp", align_bytes=64)
                     gts.append(gt)
-                nc.scalar.copy(
-                    out=gts[-1][:, g % 2, :].bitcast(F32).rearrange("p (r u) -> p r u", u=2),
-                    in_=banks[g][:].rearrange("p u r -> p r u"),
-                )
+                ev_out = gts[-1][:, g % 2, :].bitcast(F32).rearrange("p (r u) -> p r u", u=2)
+                ev_in = bank[:].rearrange("p u r -> p r u")
+                if v_helps and g % 2 == 1:
+                    nc.vector.tensor_copy(out=ev_out, in_=ev_in)
+                else:
+                    nc.scalar.copy(out=ev_out, in_=ev_in)
                 if g % 2 == 1:
                     if g == 1:
                         run(slots.get("a", []))
@@ -134,11 +150,14 @@ def tile_grucellstack_pa_kernel(tc, x, h0, gh0, w_ih, b_ih, out_0, out_1):
                         run(slots.get("c", []))
                     else:
                         run(slots.get("d", []))
+                        run(slots.get("d2", []))
                     nc.vector.quantize_mx(
                         out=codes[:, g - 1:g + 1, :].rearrange("p g r -> p (g r)").bitcast(FP8X4),
                         scales=scales[:, g - 1:g + 1, :].rearrange("p g r -> p (g r)"),
                         in_=gts[-1][:].rearrange("p g c -> p (g c)"),
                     )
+                    if g == 1:
+                        run(slots.get("m", []))
             run(slots.get("e", []))
 
         wcodes = {}
@@ -150,21 +169,21 @@ def tile_grucellstack_pa_kernel(tc, x, h0, gh0, w_ih, b_ih, out_0, out_1):
             wcodes[q] = (c_t, s_t)
             return c_t, s_t
 
-        def mx(q):
+        def mx(q, b):
             c_t, s_t = wcodes[q]
-            a_t = acc_pool.tile([P, NB, CB], F32, name="acc", tag="acc")
-            acc[q] = a_t
-            for b in range(NB):
-                for g in range(NG):
-                    nc.tensor.matmul_mx(
-                        out=a_t[:, b, :],
-                        lhsT=xc[:, g, P * b:P * (b + 1)].bitcast(FP8X4),
-                        lhsT_scale=xs[:, g, P * b:P * (b + 1)],
-                        rhs=c_t[:, g, :].bitcast(FP8X4),
-                        rhs_scale=s_t[:, g, :],
-                        start=(g == 0),
-                        stop=(g == NG - 1),
-                    )
+            if b == 0:
+                a_t = acc_pool.tile([P, NB, CB], F32, name="acc", tag="acc")
+                acc[PAIRS[q]] = a_t
+            for g in range(NG):
+                nc.tensor.matmul_mx(
+                    out=acc[PAIRS[q]][:, b, :],
+                    lhsT=xc[:, g, P * b:P * (b + 1)].bitcast(FP8X4),
+                    lhsT_scale=xs[:, g, P * b:P * (b + 1)],
+                    rhs=c_t[:, g, :].bitcast(FP8X4),
+                    rhs_scale=s_t[:, g, :],
+                    start=(g == 0),
+                    stop=(g == NG - 1),
+                )
 
         st = {}
         ALLB = slice(0, NB)
@@ -175,9 +194,6 @@ def tile_grucellstack_pa_kernel(tc, x, h0, gh0, w_ih, b_ih, out_0, out_1):
         def ghv(c, gate, bs):
             return gh_t[c // 2][:, bs, gate, cols(c)]
 
-        def bv(c, gate, bs):
-            return b_t[c // 2][:, gate, cols(c)].unsqueeze(1).to_broadcast([P, bs.stop - bs.start, CB])
-
         def tl(nm, c):
             if (nm, c) not in st:
                 t = tmp.tile([P, NB, CB], F32, name=nm, tag=nm)
@@ -185,10 +201,10 @@ def tile_grucellstack_pa_kernel(tc, x, h0, gh0, w_ih, b_ih, out_0, out_1):
             return st[(nm, c)]
 
         def pre(c, gate):
-            nc.vector.tensor_tensor(out=tl("G%d" % gate, c)[:], in0=ghv(c, gate, ALLB), in1=bv(c, gate, ALLB), op=ALU.add)
+            nc.vector.tensor_tensor(out=tl("G%d" % gate, c)[:], in0=bv(c, gate), in1=ghv(c, gate, ALLB), op=ALU.add)
 
         def e12(c, gate):
-            nc.vector.tensor_tensor(out=tl("a%d" % gate, c)[:], in0=acc[3 * c + gate][:], in1=tl("G%d" % gate, c)[:], op=ALU.add)
+            nc.vector.tensor_tensor(out=tl("a%d" % gate, c)[:], in0=acc[(gate, c)][:], in1=tl("G%d" % gate, c)[:], op=ALU.add)
 
         def s12(c, gate):
             nc.scalar.activation(out=tl("th%d" % gate, c)[:], in_=tl("a%d" % gate, c)[:], func=ACT.Tanh, scale=0.5)
@@ -196,11 +212,11 @@ def tile_grucellstack_pa_kernel(tc, x, h0, gh0, w_ih, b_ih, out_0, out_1):
         def e3(c):
             nc.vector.scalar_tensor_tensor(out=tl("w", c)[:], in0=tl("th0", c)[:], scalar=1.0, in1=ghv(c, 2, ALLB), op0=ALU.add, op1=ALU.mult)
 
-        def e4(c, bs=ALLB):
-            nc.vector.tensor_tensor(out=tl("v", c)[:, bs, :], in0=acc[3 * c + 2][:, bs, :], in1=bv(c, 2, bs), op=ALU.add)
+        def e4(c):
+            nc.vector.scalar_tensor_tensor(out=tl("t2", c)[:], in0=tl("w", c)[:], scalar=0.5, in1=bv(c, 2), op0=ALU.mult, op1=ALU.add)
 
         def e5(c, bs=ALLB):
-            nc.vector.scalar_tensor_tensor(out=tl("u", c)[:, bs, :], in0=tl("w", c)[:, bs, :], scalar=0.5, in1=tl("v", c)[:, bs, :], op0=ALU.mult, op1=ALU.add)
+            nc.vector.tensor_tensor(out=tl("u", c)[:, bs, :], in0=acc[(2, c)][:, bs, :], in1=tl("t2", c)[:, bs, :], op=ALU.add)
 
         def s3(c, bs=ALLB):
             nc.scalar.activation(out=tl("n", c)[:, bs, :], in_=tl("u", c)[:, bs, :], func=ACT.Tanh)
@@ -225,84 +241,100 @@ def tile_grucellstack_pa_kernel(tc, x, h0, gh0, w_ih, b_ih, out_0, out_1):
         def at(it, slot, fn):
             plan.setdefault(it, {}).setdefault(slot, []).append(fn)
 
-        for c in range(NCB):
-            if c == 0:
-                at(1, "e", lambda c=c: pre(c, 0))
-                at(1, "e", lambda c=c: pre(c, 1))
-                at(2, "a", lambda c=c: e12(c, 0))
-                at(2, "b", lambda c=c: e12(c, 1))
-                at(2, "s", lambda c=c: s12(c, 0))
-                at(2, "s", lambda c=c: s12(c, 1))
-                at(3, "a", lambda c=c: e4(c))
-                at(3, "b", lambda c=c: e3(c))
-                at(3, "d", lambda c=c: e5(c))
-            else:
-                if c == 1:
-                    at(3, "c", lambda c=c: pre(c, 0))
-                    at(4, "c", lambda c=c: pre(c, 1))
-                else:
-                    at(3 * c, "b", lambda c=c: pre(c, 0))
-                    at(3 * c, "d", lambda c=c: pre(c, 1))
-                at(3 * c + 1, "a", lambda c=c: e12(c, 0))
-                at(3 * c + 1, "s", lambda c=c: s12(c, 0))
-                if c < NCB - 1:
-                    at(3 * c + 2, "a", lambda c=c: e12(c, 1))
-                    at(3 * c + 2, "s", lambda c=c: s12(c, 1))
-                    at(3 * c + 2, "c", lambda c=c: e3(c))
-                    at(3 * c + 3, "a", lambda c=c: e4(c))
-                    at(3 * c + 3, "c", lambda c=c: e5(c))
-            if c < NCB - 1:
-                at(3 * c + 3, "s", lambda c=c: s3(c))
-                at(3 * c + 4, "b", lambda c=c: e6(c))
-                at(3 * c + 4, "d", lambda c=c: e7(c))
-            if c < NCB - 2:
-                at(3 * c + 5, "b", lambda c=c: e8(c))
-                at(3 * c + 5, "b", lambda c=c: store0(c))
-                if c % 2 == 1:
-                    at(3 * c + 5, "d", lambda c=c: e9(c - 1, 0, CB * (c - 1), CB * (c + 1)))
-                    at(3 * c + 7, "c", lambda c=c: e9(c, 1, CB * (c - 1), CB * (c + 1)))
+        for c in range(NCB - 2):
+            at(3 * c - 1, "pe2", lambda c=c: bias_mm(c, 0))
+            at(3 * c, "d", lambda c=c: pre(c, 0))
+            at(3 * c, "pe2", lambda c=c: bias_mm(c, 1))
+            at(3 * c + 1, "d", lambda c=c: pre(c, 1))
+            at(3 * c + 1, "a", lambda c=c: e12(c, 0))
+            at(3 * c + 1, "m", lambda c=c: s12(c, 0))
+            at(3 * c + 2, "a", lambda c=c: e12(c, 1))
+            at(3 * c + 2, "s", lambda c=c: s12(c, 1))
+            at(3 * c + 2, "c", lambda c=c: e3(c))
+            at(3 * c + 1, "pe2", lambda c=c: bias_mm(c, 2))
+            at(3 * c + 2, "d2", lambda c=c: e4(c))
+            at(3 * c + 3, "a", lambda c=c: e5(c))
+            at(3 * c + 3, "m", lambda c=c: s3(c))
+            at(3 * c + 3, "e", lambda c=c: e6(c))
+            at(3 * c + 4, "b", lambda c=c: e7(c))
+            at(3 * c + 4, "e", lambda c=c: e8(c))
+            at(3 * c + 4, "e", lambda c=c: store0(c))
+            if c % 2 == 1:
+                at(3 * c + 5, "b", lambda c=c: e9(c - 1, 0, CB * (c - 1), CB * (c + 1)))
+                at(3 * c + 5, "d", lambda c=c: e9(c, 1, CB * (c - 1), CB * (c + 1)))
+        at(11, "pe2", lambda: bias_mm(4, 0))
+        at(11, "pe2", lambda: bias_mm(5, 0))
+        at(12, "b", lambda: pre(4, 0))
+        at(12, "d", lambda: pre(5, 0))
+        at(12, "pe2", lambda: bias_mm(4, 1))
+        at(13, "a", lambda: e12(4, 0))
+        at(13, "m", lambda: s12(4, 0))
+        at(13, "d", lambda: pre(4, 1))
+        at(13, "pe2", lambda: bias_mm(4, 2))
+        at(14, "a", lambda: e12(5, 0))
+        at(14, "m", lambda: s12(5, 0))
+        at(14, "c", lambda: e3(4))
+        at(14, "d2", lambda: e4(4))
+        at(14, "pe2", lambda: bias_mm(5, 1))
+        at(15, "a", lambda: e12(4, 1))
+        at(15, "m", lambda: s12(4, 1))
+        at(15, "pe", lambda: bias_mm(5, 2))
+        at(15, "c", lambda: e3(5))
+        at(15, "d", lambda: pre(5, 1))
+        at(15, "d2", lambda: e4(5))
+        at(16, "a", lambda: e5(4))
+        at(16, "m", lambda: s3(4))
+        at(16, "d", lambda: e6(4))
+        at(16, "e", lambda: e7(4))
+        c = NCB - 1
 
-        load_pair(-1)
-        load_pair(0)
-        load_pair(1)
-        load_bias(0)
-        load_pair(2)
+        load_pair(-1, True)
+        nc.sync.dma_start(out=bias_rows[0:NCB, :].rearrange("c (g j) -> c g j", g=3), in_=b_ih.rearrange("(g c j) -> c g j", g=3, c=NCB))
+        load_pair(0, True)
+        load_pair(1, True)
         load_gh(0)
-        load_pair(3)
+        load_pair(2, True)
+        load_pair(3, False)
         load_h(0)
-        load_pair(4)
-        load_pair(5)
-        load_pair(6)
-        load_bias(1)
+        load_pair(4, False)
+        load_pair(5, False)
+        load_pair(6, False)
         load_gh(1)
         load_h(1)
 
-        stage(-1, xc, xs, True, {})
+        for i in range(NWARM):
+            idle_mm(512)
+        head = {}
+        if NWARM > 0:
+            head = {"pe": [lambda: idle_mm(512)], "pe2": [lambda: idle_mm(512)]}
+        stage(-1, xc, xs, head, True, nothing)
         c_t, s_t = new_codes(0)
-        stage(0, c_t, s_t, True, {})
+        head0 = dict(head)
+        head0["pe2"] = head.get("pe2", []) + plan[-1]["pe2"]
+        stage(0, c_t, s_t, head0, True, nothing)
 
         for it in range(NPAIR - 1):
             if it + AHEAD < NPAIR:
-                load_pair(it + AHEAD)
+                load_pair(it + AHEAD, False)
             if it == 3:
-                load_bias(2)
                 load_gh(2)
                 load_h(2)
             c_t, s_t = new_codes(it + 1)
-            stage(it + 1, c_t, s_t, it + 1 <= 2, plan.get(it, {}))
-            mx(it)
+            if SPLIT_MX:
+                stage(it + 1, c_t, s_t, plan.get(it, {}), it == 0, lambda b, it=it: mx(it, b))
+            else:
+                stage(it + 1, c_t, s_t, plan.get(it, {}), it == 0, nothing)
+                mx(it, 0)
+                mx(it, 1)
             run(plan.get(it, {}).get("s", []))
 
-        c = NCB - 1
         halves = [slice(0, 1), slice(1, 2)]
-        mx(NPAIR - 1)
+        mx(NPAIR - 1, 0)
+        mx(NPAIR - 1, 1)
         e12(c, 1)
         s12(c, 1)
-        e3(c)
         e8(c - 1)
         store0(c - 1)
-        for bs in halves:
-            e4(c, bs)
         for bs in halves:
             e5(c, bs)
         for bs in halves:

@@ -8,7 +8,6 @@ FLOPS = 2 * B * IN * 3 * L
 
 F32 = mybir.dt.float32
 BF16 = mybir.dt.bfloat16
-I32 = mybir.dt.int32
 U32 = mybir.dt.uint32
 U8 = mybir.dt.uint8
 FP8X4 = mybir.dt.float8_e4m3fn_x4
@@ -24,9 +23,6 @@ CB = 256
 NCB = L // CB
 NPAIR = 3 * NCB
 AHEAD = 7
-PAIRS = [(g, c) for c in range(NCB - 2) for g in range(3)] + [(0, 4), (0, 5), (1, 4), (2, 4), (1, 5), (2, 5)]
-SPLIT_MX = False
-NWARM = 6
 
 
 def tile_grucellstack_pa_kernel(tc, x, h0, gh0, w_ih, b_ih, out_0, out_1):
@@ -38,42 +34,39 @@ def tile_grucellstack_pa_kernel(tc, x, h0, gh0, w_ih, b_ih, out_0, out_1):
         code_pool = ctx.enter_context(tc.tile_pool(name="code", bufs=3))
         tmp = ctx.enter_context(tc.tile_pool(name="tmp", bufs=2))
         tp_pool = ctx.enter_context(tc.psum_pool(name="tp", bufs=4))
-        acc_pool = ctx.enter_context(tc.psum_pool(name="acc", bufs=2))
-        bias_pool = ctx.enter_context(tc.psum_pool(name="biasp", bufs=2))
+        acc_pool = ctx.enter_context(tc.psum_pool(name="acc", bufs=4))
         ctx.enter_context(tc.manual_schedule())
 
         zeros = const.tile([P, 1], F32, name="zeros")
         nc.vector.memset(zeros[:], 0.0)
         junk = const.tile([P, 1], F32, name="junk")
         nc.scalar.activation(out=junk[:], in_=zeros[:], func=ACT.Tanh)
-        onesw = const.tile([P, 512], BF16, name="onesw")
-        nc.gpsimd.memset(onesw[:], 1.0)
-        bias_rows = const.tile([P, 3 * CB], BF16, name="bias_rows")
-        nc.vector.memset(bias_rows[:].bitcast(I32), 0)
         ident = const.tile([P, P], F32, name="ident")
         make_identity(nc, ident[:])
-        identb = const.tile([P, P], BF16, name="identb")
-        make_identity(nc, identb[:])
 
         xc = const.tile([P, NG, 2 * P], U32, name="xc", align_bytes=64)
         xs = const.tile([P, NG, 2 * P], U8, name="xs", align_bytes=64)
-        o_all = const.tile([P, NB, L], F32, name="o_all")
-        pm = const.tile([P, 8], F32, name="pm")
+        o_ext = const.tile([P, NB * L + 8], F32, name="o_ext")
+        o_all = o_ext[:, 0:NB * L].rearrange("p (b l) -> p b l", b=NB)
+        pm = o_ext[:, NB * L:NB * L + 8]
+        nc.vector.memset(pm, 0.0)
 
         gh_v = gh0.rearrange("(b p) (g l) -> b p g l", p=P, g=3)
         h_v = h0.rearrange("(b p) l -> p b l", p=P)
+        b_v = b_ih.rearrange("(g l) -> g l", g=3)
         o0_v = out_0.rearrange("(b p) l -> p b l", p=P)
 
         raw_tiles = {}
         gh_t = {}
         h_t = {}
+        b_t = {}
 
-        def load_pair(q, split):
+        def load_pair(q, split=False):
             t = raw.tile([P, 2, IN], BF16, name="rawt", tag="raw")
             if q < 0:
                 src = x
             else:
-                n0 = PAIRS[q][0] * L + PAIRS[q][1] * CB
+                n0 = (q % 3) * L + (q // 3) * CB
                 src = w_ih[n0:n0 + 2 * P, :]
             src = src.rearrange("(j p) k -> p j k", p=P)
             if split:
@@ -82,6 +75,11 @@ def tile_grucellstack_pa_kernel(tc, x, h0, gh0, w_ih, b_ih, out_0, out_1):
             else:
                 nc.sync.dma_start(out=t[:], in_=src)
             raw_tiles[q] = t
+
+        def load_bias(k):
+            t = const.tile([P, 3, 512], BF16, name="bias%d" % k)
+            nc.sync.dma_start(out=t[:], in_=b_v[:, 512 * k:512 * (k + 1)].partition_broadcast(P))
+            b_t[k] = t
 
         def load_gh(k):
             t = const.tile([P, NB, 3, 512], BF16, name="gh%d" % k)
@@ -94,55 +92,45 @@ def tile_grucellstack_pa_kernel(tc, x, h0, gh0, w_ih, b_ih, out_0, out_1):
             nc.sync.dma_start(out=t[:], in_=h_v[:, :, 512 * k:512 * (k + 1)])
             h_t[k] = t
 
-        bias_ps = {}
-
-        def bias_mm(c, gate):
-            ps = bias_pool.tile([P, NB, CB], F32, name="bps", tag="bps")
-            nc.tensor.matmul(out=ps[:, 0, :], lhsT=identb[:, c:c + 1].to_broadcast([P, P]), rhs=bias_rows[:, CB * gate:CB * (gate + 1)], start=True, stop=True)
-            bias_ps[(c, gate)] = ps
-
-        def bv(c, gate):
-            return bias_ps[(c, gate)][:, 0:1, :].to_broadcast([P, NB, CB])
-
-        idle = acc_pool.tile([P, NB, CB], F32, name="acc", tag="acc")
-
-        def idle_mm(n):
-            nc.tensor.matmul(out=idle[:].rearrange("p b c -> p (b c)")[:, 0:n], lhsT=onesw[:, 0:P], rhs=onesw[:, 0:n], start=True, stop=True)
-
         def run(fns):
             for fn in fns:
                 fn()
 
-        def nothing(i):
-            return None
-
-        def stage(q, codes, scales, slots, v_helps, mx_half):
+        def stage(q, codes, scales, by_tile, slots):
             words = [raw_tiles[q][:, j, :].bitcast(F32) for j in range(2)]
+            banks = []
+
+            def new_bank():
+                bk = tp_pool.tile([P, 2, 2 * P], F32, name="bank", tag="tp")
+                banks.append(bk)
+
+            def tr(g, j):
+                for u in range(2):
+                    nc.tensor.transpose(
+                        banks[g][:, u, P * j:P * (j + 1)],
+                        words[j][:, 256 * g + u:256 * (g + 1):2],
+                        ident[:],
+                    )
+
+            if by_tile:
+                for g in range(NG):
+                    new_bank()
+                for j in range(2):
+                    for g in range(NG):
+                        tr(g, j)
             gts = []
             for g in range(NG):
-                bank = tp_pool.tile([P, 2, 2 * P], F32, name="bank", tag="tp")
-                for j in range(2):
-                    for u in range(2):
-                        nc.tensor.transpose(
-                            bank[:, u, P * j:P * (j + 1)],
-                            words[j][:, 256 * g + u:256 * (g + 1):2],
-                            ident[:],
-                        )
-                if g == 1:
-                    run(slots.get("pe", []))
-                    mx_half(0)
-                if g == 3:
-                    run(slots.get("pe2", []))
-                    mx_half(1)
+                if not by_tile:
+                    new_bank()
+                    tr(g, 0)
+                    tr(g, 1)
                 if g % 2 == 0:
                     gt = grp_pool.tile([P, 2, 1024], BF16, name="gt", tag="grp", align_bytes=64)
                     gts.append(gt)
-                ev_out = gts[-1][:, g % 2, :].bitcast(F32).rearrange("p (r u) -> p r u", u=2)
-                ev_in = bank[:].rearrange("p u r -> p r u")
-                if v_helps and g % 2 == 1:
-                    nc.vector.tensor_copy(out=ev_out, in_=ev_in)
-                else:
-                    nc.scalar.copy(out=ev_out, in_=ev_in)
+                nc.scalar.copy(
+                    out=gts[-1][:, g % 2, :].bitcast(F32).rearrange("p (r u) -> p r u", u=2),
+                    in_=banks[g][:].rearrange("p u r -> p r u"),
+                )
                 if g % 2 == 1:
                     if g == 1:
                         run(slots.get("a", []))
@@ -150,14 +138,11 @@ def tile_grucellstack_pa_kernel(tc, x, h0, gh0, w_ih, b_ih, out_0, out_1):
                         run(slots.get("c", []))
                     else:
                         run(slots.get("d", []))
-                        run(slots.get("d2", []))
                     nc.vector.quantize_mx(
                         out=codes[:, g - 1:g + 1, :].rearrange("p g r -> p (g r)").bitcast(FP8X4),
                         scales=scales[:, g - 1:g + 1, :].rearrange("p g r -> p (g r)"),
                         in_=gts[-1][:].rearrange("p g c -> p (g c)"),
                     )
-                    if g == 1:
-                        run(slots.get("m", []))
             run(slots.get("e", []))
 
         wcodes = {}
@@ -169,21 +154,21 @@ def tile_grucellstack_pa_kernel(tc, x, h0, gh0, w_ih, b_ih, out_0, out_1):
             wcodes[q] = (c_t, s_t)
             return c_t, s_t
 
-        def mx(q, b):
+        def mx(q):
             c_t, s_t = wcodes[q]
-            if b == 0:
-                a_t = acc_pool.tile([P, NB, CB], F32, name="acc", tag="acc")
-                acc[PAIRS[q]] = a_t
-            for g in range(NG):
-                nc.tensor.matmul_mx(
-                    out=acc[PAIRS[q]][:, b, :],
-                    lhsT=xc[:, g, P * b:P * (b + 1)].bitcast(FP8X4),
-                    lhsT_scale=xs[:, g, P * b:P * (b + 1)],
-                    rhs=c_t[:, g, :].bitcast(FP8X4),
-                    rhs_scale=s_t[:, g, :],
-                    start=(g == 0),
-                    stop=(g == NG - 1),
-                )
+            a_t = acc_pool.tile([P, NB, CB], F32, name="acc", tag="acc")
+            acc[q] = a_t
+            for b in range(NB):
+                for g in range(NG):
+                    nc.tensor.matmul_mx(
+                        out=a_t[:, b, :],
+                        lhsT=xc[:, g, P * b:P * (b + 1)].bitcast(FP8X4),
+                        lhsT_scale=xs[:, g, P * b:P * (b + 1)],
+                        rhs=c_t[:, g, :].bitcast(FP8X4),
+                        rhs_scale=s_t[:, g, :],
+                        start=(g == 0),
+                        stop=(g == NG - 1),
+                    )
 
         st = {}
         ALLB = slice(0, NB)
@@ -194,6 +179,9 @@ def tile_grucellstack_pa_kernel(tc, x, h0, gh0, w_ih, b_ih, out_0, out_1):
         def ghv(c, gate, bs):
             return gh_t[c // 2][:, bs, gate, cols(c)]
 
+        def bv(c, gate, bs):
+            return b_t[c // 2][:, gate, cols(c)].unsqueeze(1).to_broadcast([P, bs.stop - bs.start, CB])
+
         def tl(nm, c):
             if (nm, c) not in st:
                 t = tmp.tile([P, NB, CB], F32, name=nm, tag=nm)
@@ -201,10 +189,10 @@ def tile_grucellstack_pa_kernel(tc, x, h0, gh0, w_ih, b_ih, out_0, out_1):
             return st[(nm, c)]
 
         def pre(c, gate):
-            nc.vector.tensor_tensor(out=tl("G%d" % gate, c)[:], in0=bv(c, gate), in1=ghv(c, gate, ALLB), op=ALU.add)
+            nc.vector.tensor_tensor(out=tl("G%d" % gate, c)[:], in0=ghv(c, gate, ALLB), in1=bv(c, gate, ALLB), op=ALU.add)
 
         def e12(c, gate):
-            nc.vector.tensor_tensor(out=tl("a%d" % gate, c)[:], in0=acc[(gate, c)][:], in1=tl("G%d" % gate, c)[:], op=ALU.add)
+            nc.vector.tensor_tensor(out=tl("a%d" % gate, c)[:], in0=acc[3 * c + gate][:], in1=tl("G%d" % gate, c)[:], op=ALU.add)
 
         def s12(c, gate):
             nc.scalar.activation(out=tl("th%d" % gate, c)[:], in_=tl("a%d" % gate, c)[:], func=ACT.Tanh, scale=0.5)
@@ -212,11 +200,11 @@ def tile_grucellstack_pa_kernel(tc, x, h0, gh0, w_ih, b_ih, out_0, out_1):
         def e3(c):
             nc.vector.scalar_tensor_tensor(out=tl("w", c)[:], in0=tl("th0", c)[:], scalar=1.0, in1=ghv(c, 2, ALLB), op0=ALU.add, op1=ALU.mult)
 
-        def e4(c):
-            nc.vector.scalar_tensor_tensor(out=tl("t2", c)[:], in0=tl("w", c)[:], scalar=0.5, in1=bv(c, 2), op0=ALU.mult, op1=ALU.add)
+        def e4(c, bs=ALLB):
+            nc.vector.tensor_tensor(out=tl("v", c)[:, bs, :], in0=acc[3 * c + 2][:, bs, :], in1=bv(c, 2, bs), op=ALU.add)
 
         def e5(c, bs=ALLB):
-            nc.vector.tensor_tensor(out=tl("u", c)[:, bs, :], in0=acc[(2, c)][:, bs, :], in1=tl("t2", c)[:, bs, :], op=ALU.add)
+            nc.vector.scalar_tensor_tensor(out=tl("u", c)[:, bs, :], in0=tl("w", c)[:, bs, :], scalar=0.5, in1=tl("v", c)[:, bs, :], op0=ALU.mult, op1=ALU.add)
 
         def s3(c, bs=ALLB):
             nc.scalar.activation(out=tl("n", c)[:, bs, :], in_=tl("u", c)[:, bs, :], func=ACT.Tanh)
@@ -241,100 +229,84 @@ def tile_grucellstack_pa_kernel(tc, x, h0, gh0, w_ih, b_ih, out_0, out_1):
         def at(it, slot, fn):
             plan.setdefault(it, {}).setdefault(slot, []).append(fn)
 
-        for c in range(NCB - 2):
-            at(3 * c - 1, "pe2", lambda c=c: bias_mm(c, 0))
-            at(3 * c, "d", lambda c=c: pre(c, 0))
-            at(3 * c, "pe2", lambda c=c: bias_mm(c, 1))
-            at(3 * c + 1, "d", lambda c=c: pre(c, 1))
-            at(3 * c + 1, "a", lambda c=c: e12(c, 0))
-            at(3 * c + 1, "m", lambda c=c: s12(c, 0))
-            at(3 * c + 2, "a", lambda c=c: e12(c, 1))
-            at(3 * c + 2, "s", lambda c=c: s12(c, 1))
-            at(3 * c + 2, "c", lambda c=c: e3(c))
-            at(3 * c + 1, "pe2", lambda c=c: bias_mm(c, 2))
-            at(3 * c + 2, "d2", lambda c=c: e4(c))
-            at(3 * c + 3, "a", lambda c=c: e5(c))
-            at(3 * c + 3, "m", lambda c=c: s3(c))
-            at(3 * c + 3, "e", lambda c=c: e6(c))
-            at(3 * c + 4, "b", lambda c=c: e7(c))
-            at(3 * c + 4, "e", lambda c=c: e8(c))
-            at(3 * c + 4, "e", lambda c=c: store0(c))
-            if c % 2 == 1:
-                at(3 * c + 5, "b", lambda c=c: e9(c - 1, 0, CB * (c - 1), CB * (c + 1)))
-                at(3 * c + 5, "d", lambda c=c: e9(c, 1, CB * (c - 1), CB * (c + 1)))
-        at(11, "pe2", lambda: bias_mm(4, 0))
-        at(11, "pe2", lambda: bias_mm(5, 0))
-        at(12, "b", lambda: pre(4, 0))
-        at(12, "d", lambda: pre(5, 0))
-        at(12, "pe2", lambda: bias_mm(4, 1))
-        at(13, "a", lambda: e12(4, 0))
-        at(13, "m", lambda: s12(4, 0))
-        at(13, "d", lambda: pre(4, 1))
-        at(13, "pe2", lambda: bias_mm(4, 2))
-        at(14, "a", lambda: e12(5, 0))
-        at(14, "m", lambda: s12(5, 0))
-        at(14, "c", lambda: e3(4))
-        at(14, "d2", lambda: e4(4))
-        at(14, "pe2", lambda: bias_mm(5, 1))
-        at(15, "a", lambda: e12(4, 1))
-        at(15, "m", lambda: s12(4, 1))
-        at(15, "pe", lambda: bias_mm(5, 2))
-        at(15, "c", lambda: e3(5))
-        at(15, "d", lambda: pre(5, 1))
-        at(15, "d2", lambda: e4(5))
-        at(16, "a", lambda: e5(4))
-        at(16, "m", lambda: s3(4))
-        at(16, "d", lambda: e6(4))
-        at(16, "e", lambda: e7(4))
-        c = NCB - 1
+        for c in range(NCB):
+            if c == 0:
+                at(1, "e", lambda c=c: pre(c, 0))
+                at(1, "e", lambda c=c: pre(c, 1))
+                at(2, "a", lambda c=c: e12(c, 0))
+                at(2, "b", lambda c=c: e12(c, 1))
+                at(2, "s", lambda c=c: s12(c, 0))
+                at(2, "s", lambda c=c: s12(c, 1))
+                at(3, "a", lambda c=c: e4(c))
+                at(3, "b", lambda c=c: e3(c))
+                at(3, "d", lambda c=c: e5(c))
+            else:
+                if c == 1:
+                    at(3, "c", lambda c=c: pre(c, 0))
+                    at(4, "c", lambda c=c: pre(c, 1))
+                else:
+                    at(3 * c, "b", lambda c=c: pre(c, 0))
+                    at(3 * c, "d", lambda c=c: pre(c, 1))
+                at(3 * c + 1, "a", lambda c=c: e12(c, 0))
+                at(3 * c + 1, "s", lambda c=c: s12(c, 0))
+                if c < NCB - 1:
+                    at(3 * c + 2, "a", lambda c=c: e12(c, 1))
+                    at(3 * c + 2, "s", lambda c=c: s12(c, 1))
+                    at(3 * c + 2, "c", lambda c=c: e3(c))
+                    at(3 * c + 3, "a", lambda c=c: e4(c))
+                    at(3 * c + 3, "c", lambda c=c: e5(c))
+            if c < NCB - 1:
+                at(3 * c + 3, "s", lambda c=c: s3(c))
+                at(3 * c + 4, "b", lambda c=c: e6(c))
+                at(3 * c + 4, "d", lambda c=c: e7(c))
+            if c < NCB - 2:
+                at(3 * c + 5, "b", lambda c=c: e8(c))
+                at(3 * c + 5, "b", lambda c=c: store0(c))
+                if c % 2 == 1:
+                    at(3 * c + 5, "d", lambda c=c: e9(c - 1, 0, CB * (c - 1), CB * (c + 1)))
+                    at(3 * c + 7, "c", lambda c=c: e9(c, 1, CB * (c - 1), CB * (c + 1)))
 
         load_pair(-1, True)
-        nc.sync.dma_start(out=bias_rows[0:NCB, :].rearrange("c (g j) -> c g j", g=3), in_=b_ih.rearrange("(g c j) -> c g j", g=3, c=NCB))
         load_pair(0, True)
         load_pair(1, True)
-        load_gh(0)
+        load_bias(0)
         load_pair(2, True)
-        load_pair(3, False)
+        load_gh(0)
+        load_pair(3, True)
         load_h(0)
-        load_pair(4, False)
-        load_pair(5, False)
-        load_pair(6, False)
+        load_pair(4, True)
+        load_pair(5)
+        load_pair(6)
+        load_bias(1)
         load_gh(1)
         load_h(1)
 
-        for i in range(NWARM):
-            idle_mm(512)
-        head = {}
-        if NWARM > 0:
-            head = {"pe": [lambda: idle_mm(512)], "pe2": [lambda: idle_mm(512)]}
-        stage(-1, xc, xs, head, True, nothing)
+        stage(-1, xc, xs, False, {})
         c_t, s_t = new_codes(0)
-        head0 = dict(head)
-        head0["pe2"] = head.get("pe2", []) + plan[-1]["pe2"]
-        stage(0, c_t, s_t, head0, True, nothing)
+        stage(0, c_t, s_t, False, {})
 
         for it in range(NPAIR - 1):
             if it + AHEAD < NPAIR:
-                load_pair(it + AHEAD, False)
+                load_pair(it + AHEAD)
             if it == 3:
+                load_bias(2)
                 load_gh(2)
                 load_h(2)
             c_t, s_t = new_codes(it + 1)
-            if SPLIT_MX:
-                stage(it + 1, c_t, s_t, plan.get(it, {}), it == 0, lambda b, it=it: mx(it, b))
-            else:
-                stage(it + 1, c_t, s_t, plan.get(it, {}), it == 0, nothing)
-                mx(it, 0)
-                mx(it, 1)
+            stage(it + 1, c_t, s_t, False, plan.get(it, {}))
+            mx(it)
             run(plan.get(it, {}).get("s", []))
 
+        c = NCB - 1
         halves = [slice(0, 1), slice(1, 2)]
-        mx(NPAIR - 1, 0)
-        mx(NPAIR - 1, 1)
+        mx(NPAIR - 1)
         e12(c, 1)
         s12(c, 1)
+        e3(c)
         e8(c - 1)
         store0(c - 1)
+        for bs in halves:
+            e4(c, bs)
         for bs in halves:
             e5(c, bs)
         for bs in halves:
@@ -344,20 +316,18 @@ def tile_grucellstack_pa_kernel(tc, x, h0, gh0, w_ih, b_ih, out_0, out_1):
         for fn in (e6, e7, e8):
             for bs in halves:
                 fn(c, bs)
-        for b in range(NB):
-            e9(6 + b, b, CB * c, CB * (c + 1))
+        e9(6, 0, CB * c, CB * (c + 1))
         store0(c)
 
         pmx = const.tile([P, 1], F32, name="pmx")
-        nc.vector.tensor_reduce(out=pmx[:], in_=pm[:], axis=AX.X, op=ALU.max)
+        nc.vector.tensor_reduce(out=pmx[:], in_=o_ext[:, NB * L - CB:NB * L + 8], axis=AX.X, op=ALU.max, apply_absolute_value=True)
         spread = tp_pool.tile([P, 2, 2 * P], F32, name="bank", tag="tp")
         nc.tensor.transpose(spread[:, 0, 0:P], pmx[:, 0:1].to_broadcast([P, P]), ident[:])
-        amax = const.tile([P, 1], F32, name="amax")
-        nc.vector.tensor_reduce(out=amax[:], in_=spread[:, 0, 0:P], axis=AX.X, op=ALU.max)
-        rec = const.tile([P, 1], F32, name="rec")
-        nc.vector.reciprocal(out=rec[:], in_=amax[:])
+        scl = const.tile([P, 1], F32, name="scl")
+        spread_sb = const.tile([P, P], F32, name="spread_sb")
+        nc.vector.tensor_scalar(out=spread_sb[:], in0=spread[:, 0, 0:P], scalar1=1.0 / 448.0, scalar2=None, op0=ALU.mult, op1=ALU.max, accum_out=scl[:, 0:1])
         rs = const.tile([P, 1], F32, name="rs")
-        nc.vector.tensor_scalar(out=rs[:], in0=rec[:], scalar1=448.0, scalar2=None, op0=ALU.mult)
+        nc.vector.reciprocal(out=rs[:], in_=scl[:])
 
         f8a = const.tile([P, L], FP8, name="f8a")
         f8b = const.tile([P, L], FP8, name="f8b")

@@ -8,6 +8,7 @@ FLOPS = 2 * B * IN * 3 * L
 
 F32 = mybir.dt.float32
 BF16 = mybir.dt.bfloat16
+I32 = mybir.dt.int32
 U32 = mybir.dt.uint32
 U8 = mybir.dt.uint8
 FP8X4 = mybir.dt.float8_e4m3fn_x4
@@ -23,6 +24,7 @@ CB = 256
 NCB = L // CB
 NPAIR = 3 * NCB
 AHEAD = 7
+NWARM = 6
 
 
 def tile_grucellstack_pa_kernel(tc, x, h0, gh0, w_ih, b_ih, out_0, out_1):
@@ -34,15 +36,22 @@ def tile_grucellstack_pa_kernel(tc, x, h0, gh0, w_ih, b_ih, out_0, out_1):
         code_pool = ctx.enter_context(tc.tile_pool(name="code", bufs=3))
         tmp = ctx.enter_context(tc.tile_pool(name="tmp", bufs=2))
         tp_pool = ctx.enter_context(tc.psum_pool(name="tp", bufs=4))
-        acc_pool = ctx.enter_context(tc.psum_pool(name="acc", bufs=4))
+        acc_pool = ctx.enter_context(tc.psum_pool(name="acc", bufs=2))
+        bias_pool = ctx.enter_context(tc.psum_pool(name="biasp", bufs=2))
         ctx.enter_context(tc.manual_schedule())
 
         zeros = const.tile([P, 1], F32, name="zeros")
         nc.vector.memset(zeros[:], 0.0)
         junk = const.tile([P, 1], F32, name="junk")
         nc.scalar.activation(out=junk[:], in_=zeros[:], func=ACT.Tanh)
+        onesw = const.tile([P, 512], BF16, name="onesw")
+        nc.gpsimd.memset(onesw[:], 1.0)
+        bias_rows = const.tile([P, 3 * CB], BF16, name="bias_rows")
+        nc.vector.memset(bias_rows[:].bitcast(I32), 0)
         ident = const.tile([P, P], F32, name="ident")
         make_identity(nc, ident[:])
+        identb = const.tile([P, P], BF16, name="identb")
+        make_identity(nc, identb[:])
 
         xc = const.tile([P, NG, 2 * P], U32, name="xc", align_bytes=64)
         xs = const.tile([P, NG, 2 * P], U8, name="xs", align_bytes=64)
@@ -53,13 +62,11 @@ def tile_grucellstack_pa_kernel(tc, x, h0, gh0, w_ih, b_ih, out_0, out_1):
 
         gh_v = gh0.rearrange("(b p) (g l) -> b p g l", p=P, g=3)
         h_v = h0.rearrange("(b p) l -> p b l", p=P)
-        b_v = b_ih.rearrange("(g l) -> g l", g=3)
         o0_v = out_0.rearrange("(b p) l -> p b l", p=P)
 
         raw_tiles = {}
         gh_t = {}
         h_t = {}
-        b_t = {}
 
         def load_pair(q, split=False):
             t = raw.tile([P, 2, IN], BF16, name="rawt", tag="raw")
@@ -76,10 +83,12 @@ def tile_grucellstack_pa_kernel(tc, x, h0, gh0, w_ih, b_ih, out_0, out_1):
                 nc.sync.dma_start(out=t[:], in_=src)
             raw_tiles[q] = t
 
-        def load_bias(k):
-            t = const.tile([P, 3, 512], BF16, name="bias%d" % k)
-            nc.sync.dma_start(out=t[:], in_=b_v[:, 512 * k:512 * (k + 1)].partition_broadcast(P))
-            b_t[k] = t
+        bias_ps = {}
+
+        def bias_mm(c, gate):
+            ps = bias_pool.tile([P, NB, CB], F32, name="bps", tag="bps")
+            nc.tensor.matmul(out=ps[:, 0, :], lhsT=identb[:, c:c + 1].to_broadcast([P, P]), rhs=bias_rows[:, CB * gate:CB * (gate + 1)], start=True, stop=True)
+            bias_ps[(c, gate)] = ps
 
         def load_gh(k):
             t = const.tile([P, NB, 3, 512], BF16, name="gh%d" % k)
@@ -124,6 +133,8 @@ def tile_grucellstack_pa_kernel(tc, x, h0, gh0, w_ih, b_ih, out_0, out_1):
                     new_bank()
                     tr(g, 0)
                     tr(g, 1)
+                    if g % 2 == 1:
+                        run(slots.get("pe%d" % g, []))
                 if g % 2 == 0:
                     gt = grp_pool.tile([P, 2, 1024], BF16, name="gt", tag="grp", align_bytes=64)
                     gts.append(gt)
@@ -179,8 +190,8 @@ def tile_grucellstack_pa_kernel(tc, x, h0, gh0, w_ih, b_ih, out_0, out_1):
         def ghv(c, gate, bs):
             return gh_t[c // 2][:, bs, gate, cols(c)]
 
-        def bv(c, gate, bs):
-            return b_t[c // 2][:, gate, cols(c)].unsqueeze(1).to_broadcast([P, bs.stop - bs.start, CB])
+        def bv(c, gate):
+            return bias_ps[(c, gate)][:, 0:1, :].to_broadcast([P, NB, CB])
 
         def tl(nm, c):
             if (nm, c) not in st:
@@ -189,7 +200,7 @@ def tile_grucellstack_pa_kernel(tc, x, h0, gh0, w_ih, b_ih, out_0, out_1):
             return st[(nm, c)]
 
         def pre(c, gate):
-            nc.vector.tensor_tensor(out=tl("G%d" % gate, c)[:], in0=ghv(c, gate, ALLB), in1=bv(c, gate, ALLB), op=ALU.add)
+            nc.vector.tensor_tensor(out=tl("G%d" % gate, c)[:], in0=bv(c, gate), in1=ghv(c, gate, ALLB), op=ALU.add)
 
         def e12(c, gate):
             nc.vector.tensor_tensor(out=tl("a%d" % gate, c)[:], in0=acc[3 * c + gate][:], in1=tl("G%d" % gate, c)[:], op=ALU.add)
@@ -200,11 +211,11 @@ def tile_grucellstack_pa_kernel(tc, x, h0, gh0, w_ih, b_ih, out_0, out_1):
         def e3(c):
             nc.vector.scalar_tensor_tensor(out=tl("w", c)[:], in0=tl("th0", c)[:], scalar=1.0, in1=ghv(c, 2, ALLB), op0=ALU.add, op1=ALU.mult)
 
-        def e4(c, bs=ALLB):
-            nc.vector.tensor_tensor(out=tl("v", c)[:, bs, :], in0=acc[3 * c + 2][:, bs, :], in1=bv(c, 2, bs), op=ALU.add)
+        def e4(c):
+            nc.vector.scalar_tensor_tensor(out=tl("t2", c)[:], in0=tl("w", c)[:], scalar=0.5, in1=bv(c, 2), op0=ALU.mult, op1=ALU.add)
 
         def e5(c, bs=ALLB):
-            nc.vector.scalar_tensor_tensor(out=tl("u", c)[:, bs, :], in0=tl("w", c)[:, bs, :], scalar=0.5, in1=tl("v", c)[:, bs, :], op0=ALU.mult, op1=ALU.add)
+            nc.vector.tensor_tensor(out=tl("u", c)[:, bs, :], in0=acc[3 * c + 2][:, bs, :], in1=tl("t2", c)[:, bs, :], op=ALU.add)
 
         def s3(c, bs=ALLB):
             nc.scalar.activation(out=tl("n", c)[:, bs, :], in_=tl("u", c)[:, bs, :], func=ACT.Tanh)
@@ -237,16 +248,22 @@ def tile_grucellstack_pa_kernel(tc, x, h0, gh0, w_ih, b_ih, out_0, out_1):
                 at(2, "b", lambda c=c: e12(c, 1))
                 at(2, "s", lambda c=c: s12(c, 0))
                 at(2, "s", lambda c=c: s12(c, 1))
-                at(3, "a", lambda c=c: e4(c))
-                at(3, "b", lambda c=c: e3(c))
+                at(-1, "pe3", lambda c=c: bias_mm(c, 0))
+                at(0, "pe3", lambda c=c: bias_mm(c, 1))
+                at(2, "pe3", lambda c=c: bias_mm(c + 1, 0))
+                at(2, "pe3", lambda c=c: bias_mm(c, 2))
+                at(3, "a", lambda c=c: e3(c))
+                at(3, "c", lambda c=c: e4(c))
                 at(3, "d", lambda c=c: e5(c))
             else:
                 if c == 1:
-                    at(3, "c", lambda c=c: pre(c, 0))
-                    at(4, "c", lambda c=c: pre(c, 1))
+                    at(3, "b", lambda c=c: pre(c, 0))
                 else:
+                    at(3 * c - 2, "pe3", lambda c=c: bias_mm(c, 0))
                     at(3 * c, "b", lambda c=c: pre(c, 0))
-                    at(3 * c, "d", lambda c=c: pre(c, 1))
+                at(3 * c, "pe3", lambda c=c: bias_mm(c, 1))
+                at(3 * c + 1, "c", lambda c=c: pre(c, 1))
+                at(min(3 * c + 2, NPAIR - 2), "pe3", lambda c=c: bias_mm(c, 2))
                 at(3 * c + 1, "a", lambda c=c: e12(c, 0))
                 at(3 * c + 1, "s", lambda c=c: s12(c, 0))
                 if c < NCB - 1:
@@ -267,9 +284,9 @@ def tile_grucellstack_pa_kernel(tc, x, h0, gh0, w_ih, b_ih, out_0, out_1):
                     at(3 * c + 7, "c", lambda c=c: e9(c, 1, CB * (c - 1), CB * (c + 1)))
 
         load_pair(-1, True)
+        nc.sync.dma_start(out=bias_rows[0:NCB, :].rearrange("c (g j) -> c g j", g=3), in_=b_ih.rearrange("(g c j) -> c g j", g=3, c=NCB))
         load_pair(0, True)
         load_pair(1, True)
-        load_bias(0)
         load_pair(2, True)
         load_gh(0)
         load_pair(3, True)
@@ -277,19 +294,25 @@ def tile_grucellstack_pa_kernel(tc, x, h0, gh0, w_ih, b_ih, out_0, out_1):
         load_pair(4, True)
         load_pair(5)
         load_pair(6)
-        load_bias(1)
         load_gh(1)
         load_h(1)
 
-        stage(-1, xc, xs, False, {})
+        idle = acc_pool.tile([P, NB, CB], F32, name="acc", tag="acc")
+
+        def idle_mm():
+            nc.tensor.matmul(out=idle[:].rearrange("p b c -> p (b c)"), lhsT=onesw[:, 0:P], rhs=onesw[:], start=True, stop=True)
+
+        for i in range(NWARM):
+            idle_mm()
+        at(0, "pe1", idle_mm)
+        stage(-1, xc, xs, False, {"pe1": [idle_mm], "pe3": [idle_mm]})
         c_t, s_t = new_codes(0)
-        stage(0, c_t, s_t, False, {})
+        stage(0, c_t, s_t, False, {"pe1": [idle_mm], "pe3": [idle_mm] + plan[-1]["pe3"]})
 
         for it in range(NPAIR - 1):
             if it + AHEAD < NPAIR:
                 load_pair(it + AHEAD)
             if it == 3:
-                load_bias(2)
                 load_gh(2)
                 load_h(2)
             c_t, s_t = new_codes(it + 1)
@@ -305,14 +328,13 @@ def tile_grucellstack_pa_kernel(tc, x, h0, gh0, w_ih, b_ih, out_0, out_1):
         e3(c)
         e8(c - 1)
         store0(c - 1)
-        for bs in halves:
-            e4(c, bs)
+        e4(c)
+        e9(4, 0, CB * (c - 1), CB * c)
         for bs in halves:
             e5(c, bs)
         for bs in halves:
             s3(c, bs)
-        for b in range(NB):
-            e9(4 + b, b, CB * (c - 1), CB * c)
+        e9(5, 1, CB * (c - 1), CB * c)
         for fn in (e6, e7, e8):
             for bs in halves:
                 fn(c, bs)

@@ -24,7 +24,7 @@ CB = 256
 NCB = L // CB
 NPAIR = 3 * NCB
 AHEAD = 7
-NWARM = 6
+NWARM = 5
 
 
 def tile_grucellstack_pa_kernel(tc, x, h0, gh0, w_ih, b_ih, out_0, out_1):
@@ -304,10 +304,9 @@ def tile_grucellstack_pa_kernel(tc, x, h0, gh0, w_ih, b_ih, out_0, out_1):
 
         for i in range(NWARM):
             idle_mm()
-        at(0, "pe1", idle_mm)
-        stage(-1, xc, xs, False, {"pe1": [idle_mm], "pe3": [idle_mm]})
+        stage(-1, xc, xs, False, {"pe3": [idle_mm]})
         c_t, s_t = new_codes(0)
-        stage(0, c_t, s_t, False, {"pe1": [idle_mm], "pe3": [idle_mm] + plan[-1]["pe3"]})
+        stage(0, c_t, s_t, False, {"pe3": [idle_mm] + plan[-1]["pe3"]})
 
         for it in range(NPAIR - 1):
             if it + AHEAD < NPAIR:

@@ -223,6 +223,9 @@ def tile_grucellstack_pa_kernel(tc, x, h0, gh0, w_ih, b_ih, out_0, out_1):
         def e6(c, bs=ALLB):
             nc.vector.tensor_tensor(out=tl("d", c)[:, bs, :], in0=h_t[c // 2][:, bs, cols(c)], in1=tl("n", c)[:, bs, :], op=ALU.subtract)
 
+        def e6g(c):
+            nc.gpsimd.tensor_tensor(out=tl("d", c)[:], in0=h_t[c // 2][:, :, cols(c)], in1=tl("n", c)[:], op=ALU.subtract)
+
         def e7(c, bs=ALLB):
             nc.vector.scalar_tensor_tensor(out=tl("e", c)[:, bs, :], in0=tl("th1", c)[:, bs, :], scalar=1.0, in1=tl("d", c)[:, bs, :], op0=ALU.add, op1=ALU.mult)
 
@@ -274,7 +277,7 @@ def tile_grucellstack_pa_kernel(tc, x, h0, gh0, w_ih, b_ih, out_0, out_1):
                     at(3 * c + 3, "c", lambda c=c: e5(c))
             if c < NCB - 1:
                 at(3 * c + 3, "s", lambda c=c: s3(c))
-                at(3 * c + 4, "b", lambda c=c: e6(c))
+                at(3 * c + 3, "s", lambda c=c: e6g(c))
                 at(3 * c + 4, "d", lambda c=c: e7(c))
             if c < NCB - 2:
                 at(3 * c + 5, "b", lambda c=c: e8(c))

@@ -281,7 +281,7 @@ def tile_grucellstack_pa_kernel(tc, x, h0, gh0, w_ih, b_ih, out_0, out_1):
                 at(3 * c + 4, "d", lambda c=c: e7(c))
             if c < NCB - 2:
                 at(3 * c + 5, "b", lambda c=c: e8(c))
-                at(3 * c + 5, "b", lambda c=c: store0(c))
+                at(max(3 * c + 5, NPAIR - AHEAD), "b", lambda c=c: store0(c))
                 if c % 2 == 1:
                     at(3 * c + 5, "d", lambda c=c: e9(c - 1, 0, CB * (c - 1), CB * (c + 1)))
                     at(3 * c + 7, "c", lambda c=c: e9(c, 1, CB * (c - 1), CB * (c + 1)))
@@ -307,9 +307,9 @@ def tile_grucellstack_pa_kernel(tc, x, h0, gh0, w_ih, b_ih, out_0, out_1):
 
         for i in range(NWARM):
             idle_mm()
-        stage(-1, xc, xs, False, {"pe3": [idle_mm]})
+        stage(-1, xc, xs, False, {})
         c_t, s_t = new_codes(0)
-        stage(0, c_t, s_t, False, {"pe3": [idle_mm] + plan[-1]["pe3"]})
+        stage(0, c_t, s_t, False, {"pe3": plan[-1]["pe3"]})
 
         for it in range(NPAIR - 1):
             if it + AHEAD < NPAIR:

@@ -356,7 +356,10 @@ def tile_grucellstack_pa_kernel(tc, x, h0, gh0, w_ih, b_ih, out_0, out_1):
         f8a = const.tile([P, L], FP8, name="f8a")
         f8b = const.tile([P, L], FP8, name="f8b")
         nc.scalar.activation(out=f8b[:, 512:L], in_=o_all[:, 1, 512:L], func=ACT.Identity, scale=rs[:, 0:1], bias=zeros[:, 0:1], saturate=False)
-        nc.vector.tensor_scalar(out=f8a[:], in0=o_all[:, 0, :], scalar1=rs[:, 0:1], scalar2=None, op0=ALU.mult, saturate=False)
-        nc.sync.dma_start(out=out_1[0:P, :], in_=f8a[:].bitcast(U8))
+        nc.vector.tensor_scalar(out=f8a[:, 0:1024], in0=o_all[:, 0, 0:1024], scalar1=rs[:, 0:1], scalar2=None, op0=ALU.mult, saturate=False)
+        nc.sync.dma_start(out=out_1[0:P, 0:1024], in_=f8a[:, 0:1024].bitcast(U8))
+        nc.vector.tensor_scalar(out=f8a[:, 1024:L], in0=o_all[:, 0, 1024:L], scalar1=rs[:, 0:1], scalar2=None, op0=ALU.mult, saturate=False)
+        nc.sync.dma_start(out=out_1[0:P, 1024:L], in_=f8a[:, 1024:L].bitcast(U8))
         nc.vector.tensor_scalar(out=f8b[:, 0:512], in0=o_all[:, 1, 0:512], scalar1=rs[:, 0:1], scalar2=None, op0=ALU.mult, saturate=False)
-        nc.sync.dma_start(out=out_1[P:2 * P, :], in_=f8b[:].bitcast(U8))
+        nc.sync.dma_start(out=out_1[P:2 * P, 0:512], in_=f8b[:, 0:512].bitcast(U8))
+        nc.sync.dma_start(out=out_1[P:2 * P, 512:L], in_=f8b[:, 512:L].bitcast(U8))

@@ -43,7 +43,7 @@ def tile_grucellstack_pa_kernel(tc, x, h0, gh0, w_ih, b_ih, out_0, out_1):
         zeros = const.tile([P, 1], F32, name="zeros")
         nc.vector.memset(zeros[:], 0.0)
         junk = const.tile([P, 1], F32, name="junk")
-        nc.scalar.activation(out=junk[:], in_=zeros[:], func=ACT.Tanh)
+        nc.scalar.activation(out=junk[:], in_=zeros[:], func=ACT.Sigmoid)
         onesw = const.tile([P, 512], BF16, name="onesw")
         nc.gpsimd.memset(onesw[:], 1.0)
         bias_rows = const.tile([P, 3 * CB], BF16, name="bias_rows")
@@ -206,13 +206,16 @@ def tile_grucellstack_pa_kernel(tc, x, h0, gh0, w_ih, b_ih, out_0, out_1):
             nc.vector.tensor_tensor(out=tl("a%d" % gate, c)[:], in0=acc[3 * c + gate][:], in1=tl("G%d" % gate, c)[:], op=ALU.add)
 
         def s12(c, gate):
-            nc.scalar.activation(out=tl("th%d" % gate, c)[:], in_=tl("a%d" % gate, c)[:], func=ACT.Tanh, scale=0.5)
+            nc.scalar.activation(out=tl("th%d" % gate, c)[:], in_=tl("a%d" % gate, c)[:], func=ACT.Sigmoid)
 
         def e3(c):
-            nc.vector.scalar_tensor_tensor(out=tl("w", c)[:], in0=tl("th0", c)[:], scalar=1.0, in1=ghv(c, 2, ALLB), op0=ALU.add, op1=ALU.mult)
+            nc.vector.tensor_tensor(out=tl("w", c)[:], in0=tl("th0", c)[:], in1=ghv(c, 2, ALLB), op=ALU.mult)
+
+        def e3g(c):
+            nc.gpsimd.tensor_tensor(out=tl("w", c)[:], in0=tl("th0", c)[:], in1=ghv(c, 2, ALLB), op=ALU.mult)
 
         def e4(c):
-            nc.vector.scalar_tensor_tensor(out=tl("t2", c)[:], in0=tl("w", c)[:], scalar=0.5, in1=bv(c, 2), op0=ALU.mult, op1=ALU.add)
+            nc.vector.tensor_tensor(out=tl("t2", c)[:], in0=tl("w", c)[:], in1=bv(c, 2), op=ALU.add)
 
         def e5(c, bs=ALLB):
             nc.vector.tensor_tensor(out=tl("u", c)[:, bs, :], in0=acc[3 * c + 2][:, bs, :], in1=tl("t2", c)[:, bs, :], op=ALU.add)
@@ -227,10 +230,13 @@ def tile_grucellstack_pa_kernel(tc, x, h0, gh0, w_ih, b_ih, out_0, out_1):
             nc.gpsimd.tensor_tensor(out=tl("d", c)[:], in0=h_t[c // 2][:, :, cols(c)], in1=tl("n", c)[:], op=ALU.subtract)
 
         def e7(c, bs=ALLB):
-            nc.vector.scalar_tensor_tensor(out=tl("e", c)[:, bs, :], in0=tl("th1", c)[:, bs, :], scalar=1.0, in1=tl("d", c)[:, bs, :], op0=ALU.add, op1=ALU.mult)
+            nc.vector.tensor_tensor(out=tl("e", c)[:, bs, :], in0=tl("th1", c)[:, bs, :], in1=tl("d", c)[:, bs, :], op=ALU.mult)
 
         def e8(c, bs=ALLB):
-            nc.vector.scalar_tensor_tensor(out=o_all[:, bs, CB * c:CB * (c + 1)], in0=tl("e", c)[:, bs, :], scalar=0.5, in1=tl("n", c)[:, bs, :], op0=ALU.mult, op1=ALU.add)
+            nc.vector.tensor_tensor(out=o_all[:, bs, CB * c:CB * (c + 1)], in0=tl("e", c)[:, bs, :], in1=tl("n", c)[:, bs, :], op=ALU.add)
+
+        def e8g(c):
+            nc.gpsimd.tensor_tensor(out=o_all[:, :, CB * c:CB * (c + 1)], in0=tl("e", c)[:], in1=tl("n", c)[:], op=ALU.add)
 
         def store0(c):
             nc.sync.dma_start(out=o0_v[:, :, CB * c:CB * (c + 1)], in_=o_all[:, :, CB * c:CB * (c + 1)])
@@ -263,16 +269,16 @@ def tile_grucellstack_pa_kernel(tc, x, h0, gh0, w_ih, b_ih, out_0, out_1):
                     at(3, "b", lambda c=c: pre(c, 0))
                 else:
                     at(3 * c - 2, "pe3", lambda c=c: bias_mm(c, 0))
-                    at(3 * c, "b", lambda c=c: pre(c, 0))
+                    at(3 * c - 1, "b", lambda c=c: pre(c, 0))
                 at(3 * c, "pe3", lambda c=c: bias_mm(c, 1))
                 at(3 * c + 1, "c", lambda c=c: pre(c, 1))
                 at(min(3 * c + 2, NPAIR - 2), "pe3", lambda c=c: bias_mm(c, 2))
                 at(3 * c + 1, "a", lambda c=c: e12(c, 0))
                 at(3 * c + 1, "s", lambda c=c: s12(c, 0))
+                at(3 * c + 1, "s", lambda c=c: e3g(c))
                 if c < NCB - 1:
                     at(3 * c + 2, "a", lambda c=c: e12(c, 1))
                     at(3 * c + 2, "s", lambda c=c: s12(c, 1))
-                    at(3 * c + 2, "c", lambda c=c: e3(c))
                     at(3 * c + 3, "a", lambda c=c: e4(c))
                     at(3 * c + 3, "c", lambda c=c: e5(c))
             if c < NCB - 1:
@@ -280,10 +286,10 @@ def tile_grucellstack_pa_kernel(tc, x, h0, gh0, w_ih, b_ih, out_0, out_1):
                 at(3 * c + 3, "s", lambda c=c: e6g(c))
                 at(3 * c + 4, "d", lambda c=c: e7(c))
             if c < NCB - 2:
-                at(3 * c + 5, "b", lambda c=c: e8(c))
-                at(max(3 * c + 5, NPAIR - AHEAD), "b", lambda c=c: store0(c))
+                at(3 * c + 5, "d", lambda c=c: e8(c))
+                at(max(3 * c + 5, NPAIR - AHEAD), "d", lambda c=c: store0(c))
                 if c % 2 == 1:
-                    at(3 * c + 5, "d", lambda c=c: e9(c - 1, 0, CB * (c - 1), CB * (c + 1)))
+                    at(3 * c + 5, "e", lambda c=c: e9(c - 1, 0, CB * (c - 1), CB * (c + 1)))
                     at(3 * c + 7, "c", lambda c=c: e9(c, 1, CB * (c - 1), CB * (c + 1)))
 
         load_pair(-1, True)
@@ -325,17 +331,16 @@ def tile_grucellstack_pa_kernel(tc, x, h0, gh0, w_ih, b_ih, out_0, out_1):
         c = NCB - 1
         halves = [slice(0, 1), slice(1, 2)]
         mx(NPAIR - 1)
+        e8g(c - 1)
         e12(c, 1)
         s12(c, 1)
-        e3(c)
-        e8(c - 1)
-        store0(c - 1)
         e4(c)
-        e9(4, 0, CB * (c - 1), CB * c)
         for bs in halves:
             e5(c, bs)
         for bs in halves:
             s3(c, bs)
+        store0(c - 1)
+        e9(4, 0, CB * (c - 1), CB * c)
         e9(5, 1, CB * (c - 1), CB * c)
         for fn in (e6, e7, e8):
             for bs in halves:

@@ -142,9 +142,18 @@ def tile_grucellstack_pa_kernel(tc, x, h0, gh0, w_ih, b_ih, out_0, out_1):
                     out=gts[-1][:, g % 2, :].bitcast(F32).rearrange("p (r u) -> p r u", u=2),
                     in_=banks[g][:].rearrange("p u r -> p r u"),
                 )
-                if g % 2 == 1:
+                if q == NPAIR - 1 and g >= 2:
+                    if g == 3:
+                        run(slots.get("d", []))
+                    nc.vector.quantize_mx(
+                        out=codes[:, g, :].bitcast(FP8X4),
+                        scales=scales[:, g, :],
+                        in_=gts[-1][:, g % 2, :],
+                    )
+                elif g % 2 == 1:
                     if g == 1:
                         run(slots.get("a", []))
+                        run(slots.get("act1", []))
                         run(slots.get("b", []))
                         run(slots.get("c", []))
                     else:
@@ -154,6 +163,8 @@ def tile_grucellstack_pa_kernel(tc, x, h0, gh0, w_ih, b_ih, out_0, out_1):
                         scales=scales[:, g - 1:g + 1, :].rearrange("p g r -> p (g r)"),
                         in_=gts[-1][:].rearrange("p g c -> p (g c)"),
                     )
+                    if g == 1:
+                        run(slots.get("d0", []))
             run(slots.get("e", []))
 
         wcodes = {}
@@ -235,6 +246,21 @@ def tile_grucellstack_pa_kernel(tc, x, h0, gh0, w_ih, b_ih, out_0, out_1):
         def e8(c, bs=ALLB):
             nc.vector.tensor_tensor(out=o_all[:, bs, CB * c:CB * (c + 1)], in0=tl("e", c)[:, bs, :], in1=tl("n", c)[:, bs, :], op=ALU.add)
 
+        def szc(c):
+            nc.scalar.activation(out=tl("zc", c)[:], in_=tl("a1", c)[:], func=ACT.Sigmoid, scale=-1.0)
+
+        def pzg(c):
+            nc.gpsimd.tensor_tensor(out=tl("d", c)[:], in0=tl("th1", c)[:], in1=h_t[c // 2][:, :, cols(c)], op=ALU.mult)
+
+        def m7(c, bs):
+            nc.vector.tensor_tensor(out=tl("e", c)[:, bs, :], in0=tl("zc", c)[:, bs, :], in1=tl("n", c)[:, bs, :], op=ALU.mult)
+
+        def m8(c, bs):
+            nc.vector.tensor_tensor(out=o_all[:, bs, CB * c:CB * (c + 1)], in0=tl("e", c)[:, bs, :], in1=tl("d", c)[:, bs, :], op=ALU.add)
+
+        def e7g(c):
+            nc.gpsimd.tensor_tensor(out=tl("e", c)[:], in0=tl("th1", c)[:], in1=tl("d", c)[:], op=ALU.mult)
+
         def e8g(c):
             nc.gpsimd.tensor_tensor(out=o_all[:, :, CB * c:CB * (c + 1)], in0=tl("e", c)[:], in1=tl("n", c)[:], op=ALU.add)
 
@@ -274,9 +300,12 @@ def tile_grucellstack_pa_kernel(tc, x, h0, gh0, w_ih, b_ih, out_0, out_1):
                 at(3 * c + 1, "c", lambda c=c: pre(c, 1))
                 at(min(3 * c + 2, NPAIR - 2), "pe3", lambda c=c: bias_mm(c, 2))
                 at(3 * c + 1, "a", lambda c=c: e12(c, 0))
-                at(3 * c + 1, "s", lambda c=c: s12(c, 0))
-                at(3 * c + 1, "s", lambda c=c: e3g(c))
+                if c == NCB - 1:
+                    at(3 * c + 1, "act1", lambda c=c: s12(c, 0))
+                    at(3 * c + 1, "d0", lambda c=c: e3(c))
                 if c < NCB - 1:
+                    at(3 * c + 1, "s", lambda c=c: s12(c, 0))
+                    at(3 * c + 1, "s", lambda c=c: e3g(c))
                     at(3 * c + 2, "a", lambda c=c: e12(c, 1))
                     at(3 * c + 2, "s", lambda c=c: s12(c, 1))
                     at(3 * c + 3, "a", lambda c=c: e4(c))
@@ -284,13 +313,17 @@ def tile_grucellstack_pa_kernel(tc, x, h0, gh0, w_ih, b_ih, out_0, out_1):
             if c < NCB - 1:
                 at(3 * c + 3, "s", lambda c=c: s3(c))
                 at(3 * c + 3, "s", lambda c=c: e6g(c))
-                at(3 * c + 4, "d", lambda c=c: e7(c))
+                if c < NCB - 2:
+                    at(3 * c + 4, "d", lambda c=c: e7(c))
+                else:
+                    at(3 * c + 3, "s", lambda c=c: e7g(c))
+                    at(3 * c + 3, "s", lambda c=c: e8g(c))
             if c < NCB - 2:
                 at(3 * c + 5, "d", lambda c=c: e8(c))
                 at(max(3 * c + 5, NPAIR - AHEAD), "d", lambda c=c: store0(c))
                 if c % 2 == 1:
                     at(3 * c + 5, "e", lambda c=c: e9(c - 1, 0, CB * (c - 1), CB * (c + 1)))
-                    at(3 * c + 7, "c", lambda c=c: e9(c, 1, CB * (c - 1), CB * (c + 1)))
+                    at(min(3 * c + 7, NPAIR - 3), "c", lambda c=c: e9(c, 1, CB * (c - 1), CB * (c + 1)))
 
         load_pair(-1, True)
         nc.sync.dma_start(out=bias_rows[0:NCB, :].rearrange("c (g j) -> c g j", g=3), in_=b_ih.rearrange("(g c j) -> c g j", g=3, c=NCB))
@@ -331,9 +364,10 @@ def tile_grucellstack_pa_kernel(tc, x, h0, gh0, w_ih, b_ih, out_0, out_1):
         c = NCB - 1
         halves = [slice(0, 1), slice(1, 2)]
         mx(NPAIR - 1)
-        e8g(c - 1)
         e12(c, 1)
         s12(c, 1)
+        szc(c)
+        pzg(c)
         e4(c)
         for bs in halves:
             e5(c, bs)
@@ -342,7 +376,7 @@ def tile_grucellstack_pa_kernel(tc, x, h0, gh0, w_ih, b_ih, out_0, out_1):
         store0(c - 1)
         e9(4, 0, CB * (c - 1), CB * c)
         e9(5, 1, CB * (c - 1), CB * c)
-        for fn in (e6, e7, e8):
+        for fn in (m7, m8):
             for bs in halves:
                 fn(c, bs)
         e9(6, 0, CB * c, CB * (c + 1))

@@ -85,10 +85,18 @@ def tile_grucellstack_pa_kernel(tc, x, h0, gh0, w_ih, b_ih, out_0, out_1):
 
         bias_ps = {}
 
-        def bias_mm(c, gate):
-            ps = bias_pool.tile([P, NB, CB], F32, name="bps", tag="bps")
-            nc.tensor.matmul(out=ps[:, 0, :], lhsT=identb[:, c:c + 1].to_broadcast([P, P]), rhs=bias_rows[:, CB * gate:CB * (gate + 1)], start=True, stop=True)
-            bias_ps[(c, gate)] = ps
+        def bias_mm(c, gate, part):
+            if part == 0:
+                ps = bias_pool.tile([P, NB, CB], F32, name="bps", tag="bps")
+                bias_ps[(c, gate)] = ps
+            ps = bias_ps[(c, gate)]
+            nc.tensor.matmul(
+                out=ps[:, 0, P * part:P * (part + 1)],
+                lhsT=identb[:, c:c + 1].to_broadcast([P, P]),
+                rhs=bias_rows[:, CB * gate + P * part:CB * gate + P * (part + 1)],
+                start=True,
+                stop=True,
+            )
 
         def load_gh(k):
             t = const.tile([P, NB, 3, 512], BF16, name="gh%d" % k)
@@ -275,6 +283,10 @@ def tile_grucellstack_pa_kernel(tc, x, h0, gh0, w_ih, b_ih, out_0, out_1):
         def at(it, slot, fn):
             plan.setdefault(it, {}).setdefault(slot, []).append(fn)
 
+        def at_bias(it, fn):
+            at(it, "pe3", lambda: fn(0))
+            at(it, "post" if it >= 0 else "pe3", lambda: fn(1))
+
         for c in range(NCB):
             if c == 0:
                 at(1, "e", lambda c=c: pre(c, 0))
@@ -283,10 +295,10 @@ def tile_grucellstack_pa_kernel(tc, x, h0, gh0, w_ih, b_ih, out_0, out_1):
                 at(2, "b", lambda c=c: e12(c, 1))
                 at(2, "s", lambda c=c: s12(c, 0))
                 at(2, "s", lambda c=c: s12(c, 1))
-                at(-1, "pe3", lambda c=c: bias_mm(c, 0))
-                at(0, "pe3", lambda c=c: bias_mm(c, 1))
-                at(2, "pe3", lambda c=c: bias_mm(c + 1, 0))
-                at(2, "pe3", lambda c=c: bias_mm(c, 2))
+                at_bias(-1, lambda part, c=c: bias_mm(c, 0, part))
+                at_bias(0, lambda part, c=c: bias_mm(c, 1, part))
+                at_bias(2, lambda part, c=c: bias_mm(c + 1, 0, part))
+                at_bias(2, lambda part, c=c: bias_mm(c, 2, part))
                 at(3, "a", lambda c=c: e3(c))
                 at(3, "c", lambda c=c: e4(c))
                 at(3, "d", lambda c=c: e5(c))
@@ -294,11 +306,11 @@ def tile_grucellstack_pa_kernel(tc, x, h0, gh0, w_ih, b_ih, out_0, out_1):
                 if c == 1:
                     at(3, "b", lambda c=c: pre(c, 0))
                 else:
-                    at(3 * c - 2, "pe3", lambda c=c: bias_mm(c, 0))
+                    at_bias(3 * c - 2, lambda part, c=c: bias_mm(c, 0, part))
                     at(3 * c - 1, "b", lambda c=c: pre(c, 0))
-                at(3 * c, "pe3", lambda c=c: bias_mm(c, 1))
+                at_bias(3 * c, lambda part, c=c: bias_mm(c, 1, part))
                 at(3 * c + 1, "c", lambda c=c: pre(c, 1))
-                at(min(3 * c + 2, NPAIR - 2), "pe3", lambda c=c: bias_mm(c, 2))
+                at_bias(min(3 * c + 2, NPAIR - 2), lambda part, c=c: bias_mm(c, 2, part))
                 at(3 * c + 1, "a", lambda c=c: e12(c, 0))
                 if c == NCB - 1:
                     at(3 * c + 1, "act1", lambda c=c: s12(c, 0))
@@ -359,6 +371,7 @@ def tile_grucellstack_pa_kernel(tc, x, h0, gh0, w_ih, b_ih, out_0, out_1):
             c_t, s_t = new_codes(it + 1)
             stage(it + 1, c_t, s_t, False, plan.get(it, {}))
             mx(it)
+            run(plan.get(it, {}).get("post", []))
             run(plan.get(it, {}).get("s", []))
 
         c = NCB - 1

@@ -25,6 +25,7 @@ NCB = L // CB
 NPAIR = 3 * NCB
 AHEAD = 7
 NWARM = 5
+FIRST_LAID = 4
 
 
 def tile_grucellstack_pa_kernel(tc, x, h0, gh0, w_ih, b_ih, out_0, out_1):
@@ -35,6 +36,7 @@ def tile_grucellstack_pa_kernel(tc, x, h0, gh0, w_ih, b_ih, out_0, out_1):
         grp_pool = ctx.enter_context(tc.tile_pool(name="grp", bufs=4))
         code_pool = ctx.enter_context(tc.tile_pool(name="code", bufs=3))
         tmp = ctx.enter_context(tc.tile_pool(name="tmp", bufs=2))
+        lay_pool = ctx.enter_context(tc.tile_pool(name="lay", bufs=3))
         tp_pool = ctx.enter_context(tc.psum_pool(name="tp", bufs=4))
         acc_pool = ctx.enter_context(tc.psum_pool(name="acc", bufs=2))
         bias_pool = ctx.enter_context(tc.psum_pool(name="biasp", bufs=2))
@@ -113,6 +115,13 @@ def tile_grucellstack_pa_kernel(tc, x, h0, gh0, w_ih, b_ih, out_0, out_1):
             for fn in fns:
                 fn()
 
+        laid = {}
+
+        def lay(q):
+            t = lay_pool.tile([P, 2, P], F32, name="laidt", tag="laid")
+            nc.scalar.copy(out=t[:], in_=raw_tiles[q][:, 0, :].bitcast(F32)[:, 768:1024].rearrange("p (i u) -> p u i", u=2))
+            laid[q] = t
+
         def stage(q, codes, scales, by_tile, slots):
             words = [raw_tiles[q][:, j, :].bitcast(F32) for j in range(2)]
             banks = []
@@ -123,11 +132,11 @@ def tile_grucellstack_pa_kernel(tc, x, h0, gh0, w_ih, b_ih, out_0, out_1):
 
             def tr(g, j):
                 for u in range(2):
-                    nc.tensor.transpose(
-                        banks[g][:, u, P * j:P * (j + 1)],
-                        words[j][:, 256 * g + u:256 * (g + 1):2],
-                        ident[:],
-                    )
+                    if q in laid and g == 3 and j == 0:
+                        src_w = laid[q][:, u, :]
+                    else:
+                        src_w = words[j][:, 256 * g + u:256 * (g + 1):2]
+                    nc.tensor.transpose(banks[g][:, u, P * j:P * (j + 1)], src_w, ident[:])
 
             if by_tile:
                 for g in range(NG):
@@ -336,6 +345,9 @@ def tile_grucellstack_pa_kernel(tc, x, h0, gh0, w_ih, b_ih, out_0, out_1):
                 if c % 2 == 1:
                     at(3 * c + 5, "e", lambda c=c: e9(c - 1, 0, CB * (c - 1), CB * (c + 1)))
                     at(min(3 * c + 7, NPAIR - 3), "c", lambda c=c: e9(c, 1, CB * (c - 1), CB * (c + 1)))
+
+        for it in range(FIRST_LAID - 2, NPAIR - 2):
+            at(it, "s", lambda it=it: lay(it + 2))
 
         load_pair(-1, True)
         nc.sync.dma_start(out=bias_rows[0:NCB, :].rearrange("c (g j) -> c g j", g=3), in_=b_ih.rearrange("(g c j) -> c g j", g=3, c=NCB))

@@ -323,7 +323,9 @@ def tile_grucellstack_pa_kernel(tc, x, h0, gh0, w_ih, b_ih, out_0, out_1):
                 at(3 * c + 1, "a", lambda c=c: e12(c, 0))
                 if c == NCB - 1:
                     at(3 * c + 1, "act1", lambda c=c: s12(c, 0))
+                    at(3 * c + 1, "c", lambda c=c: e7(c - 1))
                     at(3 * c + 1, "d0", lambda c=c: e3(c))
+                    at(3 * c + 1, "d0", lambda c=c: e8(c - 1))
                 if c < NCB - 1:
                     at(3 * c + 1, "s", lambda c=c: s12(c, 0))
                     at(3 * c + 1, "s", lambda c=c: e3g(c))
@@ -336,9 +338,6 @@ def tile_grucellstack_pa_kernel(tc, x, h0, gh0, w_ih, b_ih, out_0, out_1):
                 at(3 * c + 3, "s", lambda c=c: e6g(c))
                 if c < NCB - 2:
                     at(3 * c + 4, "d", lambda c=c: e7(c))
-                else:
-                    at(3 * c + 3, "s", lambda c=c: e7g(c))
-                    at(3 * c + 3, "s", lambda c=c: e8g(c))
             if c < NCB - 2:
                 at(3 * c + 5, "d", lambda c=c: e8(c))
                 at(max(3 * c + 5, NPAIR - AHEAD), "d", lambda c=c: store0(c))

@@ -118,8 +118,9 @@ def tile_grucellstack_pa_kernel(tc, x, h0, gh0, w_ih, b_ih, out_0, out_1):
         laid = {}
 
         def lay(q):
-            t = lay_pool.tile([P, 2, P], F32, name="laidt", tag="laid")
-            nc.scalar.copy(out=t[:], in_=raw_tiles[q][:, 0, :].bitcast(F32)[:, 768:1024].rearrange("p (i u) -> p u i", u=2))
+            t = lay_pool.tile([P, 3, P], F32, name="laidt", tag="laid")
+            nc.scalar.copy(out=t[:, 0:2, :], in_=raw_tiles[q][:, 0, :].bitcast(F32)[:, 768:1024].rearrange("p (i u) -> p u i", u=2))
+            nc.scalar.copy(out=t[:, 2, :], in_=raw_tiles[q][:, 1, :].bitcast(F32)[:, 768:1024:2])
             laid[q] = t
 
         def stage(q, codes, scales, by_tile, slots):
@@ -132,8 +133,8 @@ def tile_grucellstack_pa_kernel(tc, x, h0, gh0, w_ih, b_ih, out_0, out_1):
 
             def tr(g, j):
                 for u in range(2):
-                    if q in laid and g == 3 and j == 0:
-                        src_w = laid[q][:, u, :]
+                    if q in laid and g == 3 and 2 * j + u < 3:
+                        src_w = laid[q][:, 2 * j + u, :]
                     else:
                         src_w = words[j][:, 256 * g + u:256 * (g + 1):2]
                     nc.tensor.transpose(banks[g][:, u, P * j:P * (j + 1)], src_w, ident[:])

from contextlib import ExitStack

import concourse.mybir as mybir
from concourse.masks import make_identity

B, IN, L = 256, 2048, 1536
FLOPS = 2 * B * IN * 3 * L

F32 = mybir.dt.float32
BF16 = mybir.dt.bfloat16
I32 = mybir.dt.int32
U32 = mybir.dt.uint32
U8 = mybir.dt.uint8
FP8X4 = mybir.dt.float8_e4m3fn_x4
FP8 = mybir.dt.float8_e4m3fn
ALU = mybir.AluOpType
ACT = mybir.ActivationFunctionType
AX = mybir.AxisListType

P = 128
NB = 2
NG = 4
CB = 256
NCB = L // CB
NPAIR = 3 * NCB
AHEAD = 7
NWARM = 5
FIRST_LAID = 4


def tile_grucellstack_pa_kernel(tc, x, h0, gh0, w_ih, b_ih, out_0, out_1):
    nc = tc.nc
    with ExitStack() as ctx:
        const = ctx.enter_context(tc.tile_pool(name="const", bufs=1))
        raw = ctx.enter_context(tc.tile_pool(name="raw", bufs=8))
        grp_pool = ctx.enter_context(tc.tile_pool(name="grp", bufs=4))
        code_pool = ctx.enter_context(tc.tile_pool(name="code", bufs=3))
        tmp = ctx.enter_context(tc.tile_pool(name="tmp", bufs=2))
        lay_pool = ctx.enter_context(tc.tile_pool(name="lay", bufs=3))
        tp_pool = ctx.enter_context(tc.psum_pool(name="tp", bufs=4))
        acc_pool = ctx.enter_context(tc.psum_pool(name="acc", bufs=2))
        bias_pool = ctx.enter_context(tc.psum_pool(name="biasp", bufs=2))
        ctx.enter_context(tc.manual_schedule())

        zeros = const.tile([P, 1], F32, name="zeros")
        nc.vector.memset(zeros[:], 0.0)
        junk = const.tile([P, 1], F32, name="junk")
        nc.scalar.activation(out=junk[:], in_=zeros[:], func=ACT.Sigmoid)
        onesw = const.tile([P, 512], BF16, name="onesw")
        nc.gpsimd.memset(onesw[:], 1.0)
        bias_rows = const.tile([P, 3 * CB], BF16, name="bias_rows")
        nc.vector.memset(bias_rows[:].bitcast(I32), 0)
        ident = const.tile([P, P], F32, name="ident")
        make_identity(nc, ident[:])
        identb = const.tile([P, P], BF16, name="identb")
        make_identity(nc, identb[:])

        xc = const.tile([P, NG, 2 * P], U32, name="xc", align_bytes=64)
        xs = const.tile([P, NG, 2 * P], U8, name="xs", align_bytes=64)
        o_ext = const.tile([P, NB * L + 8], F32, name="o_ext")
        o_all = o_ext[:, 0:NB * L].rearrange("p (b l) -> p b l", b=NB)
        pm = o_ext[:, NB * L:NB * L + 8]
        nc.vector.memset(pm, 0.0)

        gh_v = gh0.rearrange("(b p) (g l) -> b p g l", p=P, g=3)
        h_v = h0.rearrange("(b p) l -> p b l", p=P)
        o0_v = out_0.rearrange("(b p) l -> p b l", p=P)

        raw_tiles = {}
        gh_t = {}
        h_t = {}

        def load_pair(q, split=False):
            t = raw.tile([P, 2, IN], BF16, name="rawt", tag="raw")
            if q < 0:
                src = x
            else:
                n0 = (q % 3) * L + (q // 3) * CB
                src = w_ih[n0:n0 + 2 * P, :]
            src = src.rearrange("(j p) k -> p j k", p=P)
            if split:
                for s in range(2):
                    nc.sync.dma_start(out=t[:, :, 1024 * s:1024 * (s + 1)], in_=src[:, :, 1024 * s:1024 * (s + 1)])
            else:
                nc.sync.dma_start(out=t[:], in_=src)
            raw_tiles[q] = t

        bias_ps = {}

        def bias_mm(c, gate, part):
            if part == 0:
                ps = bias_pool.tile([P, NB, CB], F32, name="bps", tag="bps")
                bias_ps[(c, gate)] = ps
            ps = bias_ps[(c, gate)]
            nc.tensor.matmul(
                out=ps[:, 0, P * part:P * (part + 1)],
                lhsT=identb[:, c:c + 1].to_broadcast([P, P]),
                rhs=bias_rows[:, CB * gate + P * part:CB * gate + P * (part + 1)],
                start=True,
                stop=True,
            )

        def load_gh(k):
            t = const.tile([P, NB, 3, 512], BF16, name="gh%d" % k)
            for b in range(NB):
                nc.sync.dma_start(out=t[:, b, :, :], in_=gh_v[b, :, :, 512 * k:512 * (k + 1)])
            gh_t[k] = t

        def load_h(k):
            t = const.tile([P, NB, 512], BF16, name="h%d" % k)
            nc.sync.dma_start(out=t[:], in_=h_v[:, :, 512 * k:512 * (k + 1)])
            h_t[k] = t

        def run(fns):
            for fn in fns:
                fn()

        laid = {}

        def lay(q):
            t = lay_pool.tile([P, 3, P], F32, name="laidt", tag="laid")
            nc.scalar.copy(out=t[:, 0:2, :], in_=raw_tiles[q][:, 0, :].bitcast(F32)[:, 768:1024].rearrange("p (i u) -> p u i", u=2))
            nc.scalar.copy(out=t[:, 2, :], in_=raw_tiles[q][:, 1, :].bitcast(F32)[:, 768:1024:2])
            laid[q] = t

        def stage(q, codes, scales, by_tile, slots):
            words = [raw_tiles[q][:, j, :].bitcast(F32) for j in range(2)]
            banks = []

            def new_bank():
                bk = tp_pool.tile([P, 2, 2 * P], F32, name="bank", tag="tp")
                banks.append(bk)

            def tr(g, j):
                for u in range(2):
                    if q in laid and g == 3 and 2 * j + u < 3:
                        src_w = laid[q][:, 2 * j + u, :]
                    else:
                        src_w = words[j][:, 256 * g + u:256 * (g + 1):2]
                    nc.tensor.transpose(banks[g][:, u, P * j:P * (j + 1)], src_w, ident[:])

            if by_tile:
                for g in range(NG):
                    new_bank()
                for j in range(2):
                    for g in range(NG):
                        tr(g, j)
            gts = []
            for g in range(NG):
                if not by_tile:
                    new_bank()
                    tr(g, 0)
                    tr(g, 1)
                    if g % 2 == 1:
                        run(slots.get("pe%d" % g, []))
                if g % 2 == 0:
                    gt = grp_pool.tile([P, 2, 1024], BF16, name="gt", tag="grp", align_bytes=64)
                    gts.append(gt)
                nc.scalar.copy(
                    out=gts[-1][:, g % 2, :].bitcast(F32).rearrange("p (r u) -> p r u", u=2),
                    in_=banks[g][:].rearrange("p u r -> p r u"),
                )
                if q == NPAIR - 1 and g >= 2:
                    if g == 3:
                        run(slots.get("d", []))
                    nc.vector.quantize_mx(
                        out=codes[:, g, :].bitcast(FP8X4),
                        scales=scales[:, g, :],
                        in_=gts[-1][:, g % 2, :],
                    )
                elif g % 2 == 1:
                    if g == 1:
                        run(slots.get("a", []))
                        run(slots.get("act1", []))
                        run(slots.get("b", []))
                        run(slots.get("c", []))
                    else:
                        run(slots.get("d", []))
                    nc.vector.quantize_mx(
                        out=codes[:, g - 1:g + 1, :].rearrange("p g r -> p (g r)").bitcast(FP8X4),
                        scales=scales[:, g - 1:g + 1, :].rearrange("p g r -> p (g r)"),
                        in_=gts[-1][:].rearrange("p g c -> p (g c)"),
                    )
                    if g == 1:
                        run(slots.get("d0", []))
            run(slots.get("e", []))

        wcodes = {}
        acc = {}

        def new_codes(q):
            c_t = code_pool.tile([P, NG, 2 * P], U32, name="wc", tag="wc", align_bytes=64)
            s_t = code_pool.tile([P, NG, 2 * P], U8, name="ws", tag="ws", align_bytes=64)
            wcodes[q] = (c_t, s_t)
            return c_t, s_t

        def mx(q):
            c_t, s_t = wcodes[q]
            a_t = acc_pool.tile([P, NB, CB], F32, name="acc", tag="acc")
            acc[q] = a_t
            for b in range(NB):
                for g in range(NG):
                    nc.tensor.matmul_mx(
                        out=a_t[:, b, :],
                        lhsT=xc[:, g, P * b:P * (b + 1)].bitcast(FP8X4),
                        lhsT_scale=xs[:, g, P * b:P * (b + 1)],
                        rhs=c_t[:, g, :].bitcast(FP8X4),
                        rhs_scale=s_t[:, g, :],
                        start=(g == 0),
                        stop=(g == NG - 1),
                    )

        st = {}
        ALLB = slice(0, NB)

        def cols(c):
            return slice(CB * (c % 2), CB * (c % 2) + CB)

        def ghv(c, gate, bs):
            return gh_t[c // 2][:, bs, gate, cols(c)]

        def bv(c, gate):
            return bias_ps[(c, gate)][:, 0:1, :].to_broadcast([P, NB, CB])

        def tl(nm, c):
            if (nm, c) not in st:
                t = tmp.tile([P, NB, CB], F32, name=nm, tag=nm)
                st[(nm, c)] = t
            return st[(nm, c)]

        def pre(c, gate):
            nc.vector.tensor_tensor(out=tl("G%d" % gate, c)[:], in0=bv(c, gate), in1=ghv(c, gate, ALLB), op=ALU.add)

        def e12(c, gate):
            nc.vector.tensor_tensor(out=tl("a%d" % gate, c)[:], in0=acc[3 * c + gate][:], in1=tl("G%d" % gate, c)[:], op=ALU.add)

        def s12(c, gate):
            nc.scalar.activation(out=tl("th%d" % gate, c)[:], in_=tl("a%d" % gate, c)[:], func=ACT.Sigmoid)

        def e3(c):
            nc.vector.tensor_tensor(out=tl("w", c)[:], in0=tl("th0", c)[:], in1=ghv(c, 2, ALLB), op=ALU.mult)

        def e3g(c):
            nc.gpsimd.tensor_tensor(out=tl("w", c)[:], in0=tl("th0", c)[:], in1=ghv(c, 2, ALLB), op=ALU.mult)

        def e4(c):
            nc.vector.tensor_tensor(out=tl("t2", c)[:], in0=tl("w", c)[:], in1=bv(c, 2), op=ALU.add)

        def e5(c, bs=ALLB):
            nc.vector.tensor_tensor(out=tl("u", c)[:, bs, :], in0=acc[3 * c + 2][:, bs, :], in1=tl("t2", c)[:, bs, :], op=ALU.add)

        def s3(c, bs=ALLB):
            nc.scalar.activation(out=tl("n", c)[:, bs, :], in_=tl("u", c)[:, bs, :], func=ACT.Tanh)

        def e6(c, bs=ALLB):
            nc.vector.tensor_tensor(out=tl("d", c)[:, bs, :], in0=h_t[c // 2][:, bs, cols(c)], in1=tl("n", c)[:, bs, :], op=ALU.subtract)

        def e6g(c):
            nc.gpsimd.tensor_tensor(out=tl("d", c)[:], in0=h_t[c // 2][:, :, cols(c)], in1=tl("n", c)[:], op=ALU.subtract)

        def e7(c, bs=ALLB):
            nc.vector.tensor_tensor(out=tl("e", c)[:, bs, :], in0=tl("th1", c)[:, bs, :], in1=tl("d", c)[:, bs, :], op=ALU.mult)

        def e8(c, bs=ALLB):
            nc.vector.tensor_tensor(out=o_all[:, bs, CB * c:CB * (c + 1)], in0=tl("e", c)[:, bs, :], in1=tl("n", c)[:, bs, :], op=ALU.add)

        def szc(c):
            nc.scalar.activation(out=tl("zc", c)[:], in_=tl("a1", c)[:], func=ACT.Sigmoid, scale=-1.0)

        def pzg(c):
            nc.gpsimd.tensor_tensor(out=tl("d", c)[:], in0=tl("th1", c)[:], in1=h_t[c // 2][:, :, cols(c)], op=ALU.mult)

        def m7(c, bs):
            nc.vector.tensor_tensor(out=tl("e", c)[:, bs, :], in0=tl("zc", c)[:, bs, :], in1=tl("n", c)[:, bs, :], op=ALU.mult)

        def m8(c, bs):
            nc.vector.tensor_tensor(out=o_all[:, bs, CB * c:CB * (c + 1)], in0=tl("e", c)[:, bs, :], in1=tl("d", c)[:, bs, :], op=ALU.add)

        def e7g(c):
            nc.gpsimd.tensor_tensor(out=tl("e", c)[:], in0=tl("th1", c)[:], in1=tl("d", c)[:], op=ALU.mult)

        def e8g(c):
            nc.gpsimd.tensor_tensor(out=o_all[:, :, CB * c:CB * (c + 1)], in0=tl("e", c)[:], in1=tl("n", c)[:], op=ALU.add)

        def store0(c):
            nc.sync.dma_start(out=o0_v[:, :, CB * c:CB * (c + 1)], in_=o_all[:, :, CB * c:CB * (c + 1)])

        def e9(col, b, lo, hi):
            nc.vector.tensor_reduce(out=pm[:, col:col + 1], in_=o_all[:, b, lo:hi], axis=AX.X, op=ALU.max, apply_absolute_value=True)

        plan = {}

        def at(it, slot, fn):
            plan.setdefault(it, {}).setdefault(slot, []).append(fn)

        def at_bias(it, fn):
            at(it, "pe3", lambda: fn(0))
            at(it, "post" if it >= 0 else "pe3", lambda: fn(1))

        for c in range(NCB):
            if c == 0:
                at(1, "e", lambda c=c: pre(c, 0))
                at(1, "e", lambda c=c: pre(c, 1))
                at(2, "a", lambda c=c: e12(c, 0))
                at(2, "b", lambda c=c: e12(c, 1))
                at(2, "s", lambda c=c: s12(c, 0))
                at(2, "s", lambda c=c: s12(c, 1))
                at_bias(-1, lambda part, c=c: bias_mm(c, 0, part))
                at_bias(0, lambda part, c=c: bias_mm(c, 1, part))
                at_bias(2, lambda part, c=c: bias_mm(c + 1, 0, part))
                at_bias(2, lambda part, c=c: bias_mm(c, 2, part))
                at(3, "a", lambda c=c: e3(c))
                at(3, "c", lambda c=c: e4(c))
                at(3, "d", lambda c=c: e5(c))
            else:
                if c == 1:
                    at(3, "b", lambda c=c: pre(c, 0))
                else:
                    at_bias(3 * c - 2, lambda part, c=c: bias_mm(c, 0, part))
                    at(3 * c - 1, "b", lambda c=c: pre(c, 0))
                at_bias(3 * c, lambda part, c=c: bias_mm(c, 1, part))
                at(3 * c + 1, "c", lambda c=c: pre(c, 1))
                at_bias(min(3 * c + 2, NPAIR - 2), lambda part, c=c: bias_mm(c, 2, part))
                at(3 * c + 1, "a", lambda c=c: e12(c, 0))
                if c == NCB - 1:
                    at(3 * c + 1, "act1", lambda c=c: s12(c, 0))
                    at(3 * c + 1, "c", lambda c=c: e7(c - 1))
                    at(3 * c + 1, "d0", lambda c=c: e3(c))
                    at(3 * c + 1, "d0", lambda c=c: e8(c - 1))
                if c < NCB - 1:
                    at(3 * c + 1, "s", lambda c=c: s12(c, 0))
                    at(3 * c + 1, "s", lambda c=c: e3g(c))
                    at(3 * c + 2, "a", lambda c=c: e12(c, 1))
                    at(3 * c + 2, "s", lambda c=c: s12(c, 1))
                    at(3 * c + 3, "a", lambda c=c: e4(c))
                    at(3 * c + 3, "c", lambda c=c: e5(c))
            if c < NCB - 1:
                at(3 * c + 3, "s", lambda c=c: s3(c))
                at(3 * c + 3, "s", lambda c=c: e6g(c))
                if c < NCB - 2:
                    at(3 * c + 4, "d", lambda c=c: e7(c))
            if c < NCB - 2:
                at(3 * c + 5, "d", lambda c=c: e8(c))
                at(max(3 * c + 5, NPAIR - AHEAD), "d", lambda c=c: store0(c))
                if c % 2 == 1:
                    at(3 * c + 5, "e", lambda c=c: e9(c - 1, 0, CB * (c - 1), CB * (c + 1)))
                    at(min(3 * c + 7, NPAIR - 3), "c", lambda c=c: e9(c, 1, CB * (c - 1), CB * (c + 1)))

        for it in range(FIRST_LAID - 2, NPAIR - 2):
            at(it, "s", lambda it=it: lay(it + 2))

        load_pair(-1, True)
        nc.sync.dma_start(out=bias_rows[0:NCB, :].rearrange("c (g j) -> c g j", g=3), in_=b_ih.rearrange("(g c j) -> c g j", g=3, c=NCB))
        load_pair(0, True)
        load_pair(1, True)
        load_pair(2, True)
        load_gh(0)
        load_pair(3, True)
        load_h(0)
        load_pair(4, True)
        load_pair(5)
        load_pair(6)
        load_gh(1)
        load_h(1)

        idle = acc_pool.tile([P, NB, CB], F32, name="acc", tag="acc")

        def idle_mm():
            nc.tensor.matmul(out=idle[:].rearrange("p b c -> p (b c)"), lhsT=onesw[:, 0:P], rhs=onesw[:], start=True, stop=True)

        for i in range(NWARM):
            idle_mm()
        stage(-1, xc, xs, False, {})
        c_t, s_t = new_codes(0)
        stage(0, c_t, s_t, False, {"pe3": plan[-1]["pe3"]})

        for it in range(NPAIR - 1):
            if it + AHEAD < NPAIR:
                load_pair(it + AHEAD)
            if it == 3:
                load_gh(2)
                load_h(2)
            c_t, s_t = new_codes(it + 1)
            stage(it + 1, c_t, s_t, False, plan.get(it, {}))
            mx(it)
            run(plan.get(it, {}).get("post", []))
            run(plan.get(it, {}).get("s", []))

        c = NCB - 1
        halves = [slice(0, 1), slice(1, 2)]
        mx(NPAIR - 1)
        e12(c, 1)
        s12(c, 1)
        szc(c)
        pzg(c)
        e4(c)
        for bs in halves:
            e5(c, bs)
        for bs in halves:
            s3(c, bs)
        store0(c - 1)
        e9(4, 0, CB * (c - 1), CB * c)
        e9(5, 1, CB * (c - 1), CB * c)
        for fn in (m7, m8):
            for bs in halves:
                fn(c, bs)
        e9(6, 0, CB * c, CB * (c + 1))
        store0(c)

        pmx = const.tile([P, 1], F32, name="pmx")
        nc.vector.tensor_reduce(out=pmx[:], in_=o_ext[:, NB * L - CB:NB * L + 8], axis=AX.X, op=ALU.max, apply_absolute_value=True)
        spread = tp_pool.tile([P, 2, 2 * P], F32, name="bank", tag="tp")
        nc.tensor.transpose(spread[:, 0, 0:P], pmx[:, 0:1].to_broadcast([P, P]), ident[:])
        scl = const.tile([P, 1], F32, name="scl")
        spread_sb = const.tile([P, P], F32, name="spread_sb")
        nc.vector.tensor_scalar(out=spread_sb[:], in0=spread[:, 0, 0:P], scalar1=1.0 / 448.0, scalar2=None, op0=ALU.mult, op1=ALU.max, accum_out=scl[:, 0:1])
        rs = const.tile([P, 1], F32, name="rs")
        nc.vector.reciprocal(out=rs[:], in_=scl[:])

        f8a = const.tile([P, L], FP8, name="f8a")
        f8b = const.tile([P, L], FP8, name="f8b")
        nc.scalar.activation(out=f8b[:, 512:L], in_=o_all[:, 1, 512:L], func=ACT.Identity, scale=rs[:, 0:1], bias=zeros[:, 0:1], saturate=False)
        nc.vector.tensor_scalar(out=f8a[:, 0:1024], in0=o_all[:, 0, 0:1024], scalar1=rs[:, 0:1], scalar2=None, op0=ALU.mult, saturate=False)
        nc.sync.dma_start(out=out_1[0:P, 0:1024], in_=f8a[:, 0:1024].bitcast(U8))
        nc.vector.tensor_scalar(out=f8a[:, 1024:L], in0=o_all[:, 0, 1024:L], scalar1=rs[:, 0:1], scalar2=None, op0=ALU.mult, saturate=False)
        nc.sync.dma_start(out=out_1[0:P, 1024:L], in_=f8a[:, 1024:L].bitcast(U8))
        nc.vector.tensor_scalar(out=f8b[:, 0:512], in0=o_all[:, 1, 0:512], scalar1=rs[:, 0:1], scalar2=None, op0=ALU.mult, saturate=False)
        nc.sync.dma_start(out=out_1[P:2 * P, 0:512], in_=f8b[:, 0:512].bitcast(U8))
        nc.sync.dma_start(out=out_1[P:2 * P, 512:L], in_=f8b[:, 512:L].bitcast(U8))
